import numpy as np
import ml_dtypes


def mxq(x, axis, fmt="e4m3"):
    dtype, down = {"e4m3": (ml_dtypes.float8_e4m3fn, 7), "e5m2": (ml_dtypes.float8_e5m2, 14)}[fmt]
    v = np.moveaxis(np.asarray(x, np.float32).astype(ml_dtypes.bfloat16).astype(np.float64), axis, -1)
    blocks = v.reshape(v.shape[:-1] + (-1, 32))
    amax = np.abs(blocks).max(-1, keepdims=True)
    byte = np.maximum(np.where(amax > 0, np.frexp(amax)[1] - 1 + 127, 0) - down, 1)
    scale = np.exp2(byte - 127.0)
    codes = (blocks / scale).astype(np.float32).astype(dtype).astype(np.float64)
    return np.moveaxis((codes * scale).reshape(v.shape), -1, axis)


WIDE = False


def mx_kscale(k):
    if not WIDE:
        return np.ones(k)
    levels = np.array([10, -10, 5, -5, 0])
    a = np.random.permutation(np.resize(levels, k // 512 * 4)).reshape(k // 512, 4)
    idx = np.arange(k)
    return np.exp2(a[idx // 512, idx % 128 // 32])


BF16 = ml_dtypes.bfloat16


def bf(x):
    return np.asarray(x, np.float32).astype(BF16)


def f64(x):
    return np.asarray(x).astype(np.float64)


B, N, F_IN, F_HID, F_OUT = 4, 1024, 512, 512, 512


def normalize_adj(adj):
    colsum = adj.sum(axis=1)
    safe = np.where(colsum > 0, colsum, 1.0)
    r = np.where(colsum > 0, safe ** -0.5, 0.0)
    return r[:, :, None] * adj.transpose(0, 2, 1) * r[:, None, :]


def setup_inputs():
    s = mx_kscale(F_IN)
    keep = np.random.random((B, 1, N)) >= 0.05
    return {"batch_graph": bf(np.random.standard_normal((B, N, F_IN)) * s),
            "adj": bf(np.random.random((B, N, N)) * keep),
            "W1": bf(np.random.standard_normal((F_IN, F_HID)) * 0.3 * np.sqrt(N / F_IN) / s[:, None]),
            "b1": bf(np.random.standard_normal(F_HID) * 0.2)}


def reference(batch_graph, adj, W1, b1):
    a = normalize_adj(f64(adj))
    h = mxq(f64(batch_graph), 2, "e4m3") @ mxq(f64(W1), 0, "e4m3")
    y = (mxq(a, 2, "e4m3") @ mxq(h, 1, "e4m3")) + f64(b1)
    return np.maximum(y, 0.0)

@@ -1,0 +1,231 @@
+from contextlib import ExitStack
+
+import concourse.mybir as mybir
+from concourse.masks import make_identity
+
+F32 = mybir.dt.float32
+BF16 = mybir.dt.bfloat16
+U32 = mybir.dt.uint32
+U8 = mybir.dt.uint8
+FP8X4 = mybir.dt.float8_e4m3fn_x4
+ALU = mybir.AluOpType
+ACT = mybir.ActivationFunctionType
+
+P = 128
+PACK = 4
+GRAPHS = 4
+NODES = 1024
+F_IN = 512
+F_OUT = 512
+BLOCKS = NODES // P
+PASSES = NODES // (P * PACK)
+BANK = 512
+HALVES = NODES // BANK
+ONES_COLS = 32
+SCALAR_PLANES = 1
+STORE_BLOCKS = 2
+
+FLOPS = 2 * GRAPHS * NODES * F_IN * F_OUT + 2 * GRAPHS * NODES * NODES * F_OUT
+
+
+def tile_gcn_pa_kernel(tc, batch_graph, adj, W1, b1, out):
+    nc = tc.nc
+    with ExitStack() as ctx:
+        consts = ctx.enter_context(tc.tile_pool(name="consts", bufs=1))
+        inputs = ctx.enter_context(tc.tile_pool(name="inputs", bufs=GRAPHS))
+        work = ctx.enter_context(tc.tile_pool(name="work", bufs=2))
+        psum = ctx.enter_context(tc.psum_pool(name="psum", bufs=2))
+
+        adj_sb = [inputs.tile([P, BLOCKS, NODES], BF16, name="adj_sb", tag="adj_sb") for g in range(GRAPHS)]
+        x_sb = [inputs.tile([P, BLOCKS, F_IN], BF16, name="x_sb", tag="x_sb") for g in range(GRAPHS)]
+        w_sb = consts.tile([P, PACK, F_OUT], BF16, name="w_sb")
+        bias_bf = consts.tile([P, F_OUT], BF16, name="bias_bf")
+
+        def load_adj(g):
+            for c in range(PASSES):
+                rows = adj[g, c * P * PACK : (c + 1) * P * PACK, :]
+                nc.sync.dma_start(
+                    out=adj_sb[g][:, c * PACK : (c + 1) * PACK, :],
+                    in_=rows.rearrange("(t p) i -> p t i", p=P),
+                )
+
+        def load_x(g):
+            nc.sync.dma_start(out=x_sb[g][:], in_=batch_graph[g].rearrange("(b p) k -> p b k", p=P))
+
+        load_adj(0)
+        nc.sync.dma_start(
+            out=w_sb[:].rearrange("q (u e) f -> q u (e f)", u=2),
+            in_=W1.rearrange("(u q e) f -> q u (e f)", u=2, e=2),
+        )
+        load_x(0)
+        nc.sync.dma_start(out=bias_bf[:], in_=b1.partition_broadcast(P))
+        for g in range(1, GRAPHS):
+            load_adj(g)
+            load_x(g)
+
+        warm = consts.tile([P, 1], F32, name="warm")
+        nc.vector.memset(warm[:], 1.0)
+        nc.scalar.sqrt(out=warm[:], in_=warm[:])
+        ones = consts.tile([P, ONES_COLS], BF16, name="ones")
+        nc.vector.memset(ones[:], 1.0)
+        ident = consts.tile([P, P], F32, name="ident")
+        make_identity(nc, ident[:])
+
+        w_grouped = consts.tile([P, F_OUT, PACK], BF16, name="w_grouped", align_bytes=64)
+        w_codes = consts.tile([P, F_OUT], U32, name="w_codes", align_bytes=64)
+        w_scales = consts.tile([P, F_OUT], U8, name="w_scales", align_bytes=64)
+        nc.vector.tensor_copy(out=w_grouped[:], in_=w_sb[:].rearrange("q t f -> q f t"))
+        nc.vector.quantize_mx(
+            out=w_codes[:].bitcast(FP8X4),
+            scales=w_scales[:],
+            in_=w_grouped[:].rearrange("q f t -> q (f t)"),
+        )
+        bias = consts.tile([P, F_OUT], F32, name="bias")
+        nc.vector.tensor_copy(out=bias[:], in_=bias_bf[:])
+
+        for g in range(GRAPHS):
+            colsum = psum.tile([P, BLOCKS, ONES_COLS], F32, name="colsum", tag="plain")
+            for nb in range(BLOCKS):
+                for mb in range(BLOCKS):
+                    nc.tensor.matmul(
+                        out=colsum[:, nb, :],
+                        lhsT=adj_sb[g][:, mb, nb * P : (nb + 1) * P],
+                        rhs=ones[:],
+                        start=(mb == 0),
+                        stop=(mb == BLOCKS - 1),
+                    )
+            sums = colsum[:, :, 0]
+            is_zero = work.tile([P, BLOCKS], F32, name="is_zero")
+            safe = work.tile([P, BLOCKS], F32, name="safe")
+            root = work.tile([P, BLOCKS], F32, name="root")
+            inv_root = work.tile([P, BLOCKS], F32, name="inv_root")
+            r_col = work.tile([P, BLOCKS], F32, name="r_col")
+            nc.vector.tensor_single_scalar(out=is_zero[:], in_=sums, scalar=0.0, op=ALU.is_le)
+            nc.vector.tensor_tensor(out=safe[:], in0=sums, in1=is_zero[:], op=ALU.add)
+            nc.scalar.sqrt(out=root[:], in_=safe[:])
+            nc.vector.reciprocal(out=inv_root[:], in_=root[:])
+            nc.vector.scalar_tensor_tensor(
+                out=r_col[:], in0=sums, scalar=0.0, in1=inv_root[:], op0=ALU.is_gt, op1=ALU.mult
+            )
+
+            repeated = work.tile([P, BLOCKS, P], F32, name="repeated")
+            nc.gpsimd.tensor_scalar(
+                out=repeated[:],
+                in0=r_col[:].unsqueeze(2).to_broadcast([P, BLOCKS, P]),
+                scalar1=1.0,
+                scalar2=0.0,
+                op0=ALU.mult,
+                op1=ALU.add,
+            )
+            r_rows = []
+            for hf in range(HALVES):
+                r_row = psum.tile([P, BANK], F32, name="r_row", tag="r_row")
+                for k in range(BANK // P):
+                    nc.tensor.transpose(r_row[:, k * P : (k + 1) * P], repeated[:, hf * (BANK // P) + k, :], ident[:])
+                r_rows.append(r_row)
+
+            x_codes = work.tile([P, NODES], U32, name="x_codes", align_bytes=64)
+            x_scales = work.tile([P, NODES], U8, name="x_scales", align_bytes=64)
+            for hf in range(HALVES):
+                x_grouped = work.tile([P, BANK * PACK], BF16, name="x_grouped", align_bytes=64)
+                x_words = x_grouped[:].bitcast(F32).rearrange("q (n u) -> q n u", u=2)
+                for pair in range(2):
+                    x_t = psum.tile([P, 2, 2, P], F32, name="x_t", tag="plain")
+                    for i in range(2):
+                        words = x_sb[g][:, 4 * hf + 2 * pair + i, :].bitcast(F32)
+                        for u in range(2):
+                            nc.tensor.transpose(x_t[:, i, u, :], words[:, u * P : (u + 1) * P], ident[:])
+                    nc.scalar.copy(
+                        out=x_words[:, pair * 2 * P : (pair + 1) * 2 * P, :].rearrange("q (i n) u -> q i n u", i=2),
+                        in_=x_t[:].rearrange("q i u n -> q i n u"),
+                    )
+                cols = slice(hf * BANK, (hf + 1) * BANK)
+                nc.vector.quantize_mx(out=x_codes[:, cols].bitcast(FP8X4), scales=x_scales[:, cols], in_=x_grouped[:])
+
+            h_codes = work.tile([P, PASSES, F_OUT], U32, name="h_codes", align_bytes=64)
+            h_scales = work.tile([P, PASSES, F_OUT], U8, name="h_scales", align_bytes=64)
+            for c in range(PASSES):
+                h_grouped = work.tile([P, F_OUT, PACK], BF16, name="h_grouped", align_bytes=64)
+                for fq in range(F_OUT // P):
+                    f_cols = slice(fq * P, (fq + 1) * P)
+                    h_acc = psum.tile([P, PACK, P], F32, name="h_acc", tag="h_acc")
+                    for t in range(PACK):
+                        n_cols = slice((c * PACK + t) * P, (c * PACK + t + 1) * P)
+                        nc.tensor.matmul_mx(
+                            out=h_acc[:, t, :],
+                            lhsT=x_codes[:, n_cols].bitcast(FP8X4),
+                            lhsT_scale=x_scales[:, n_cols],
+                            rhs=w_codes[:, f_cols].bitcast(FP8X4),
+                            rhs_scale=w_scales[:, f_cols],
+                            start=True,
+                            stop=True,
+                        )
+                    nc.scalar.copy(out=h_grouped[:, f_cols, :], in_=h_acc[:].rearrange("p t f -> p f t"))
+                nc.vector.quantize_mx(
+                    out=h_codes[:, c, :].bitcast(FP8X4),
+                    scales=h_scales[:, c, :],
+                    in_=h_grouped[:].rearrange("p f t -> p (f t)"),
+                )
+
+            a_codes = work.tile([P, PASSES, NODES], U32, name="a_codes", align_bytes=64)
+            a_scales = work.tile([P, PASSES, NODES], U8, name="a_scales", align_bytes=64)
+            scaled = []
+            for c in range(PASSES):
+                planes = work.tile([P, PACK, NODES], F32, name="planes")
+                for t in range(PACK):
+                    b = c * PACK + t
+                    if t < SCALAR_PLANES:
+                        nc.scalar.activation(
+                            out=planes[:, t, :], in_=adj_sb[g][:, b, :], func=ACT.Copy, scale=r_col[:, b : b + 1]
+                        )
+                    else:
+                        nc.gpsimd.tensor_scalar(
+                            out=planes[:, t, :],
+                            in0=adj_sb[g][:, b, :],
+                            scalar1=r_col[:, b : b + 1],
+                            scalar2=0.0,
+                            op0=ALU.mult,
+                            op1=ALU.add,
+                        )
+                scaled.append(planes)
+
+            steps = [(c, hf) for c in range(PASSES) for hf in range(HALVES)]
+            a_grouped = {}
+            for k in range(len(steps) + 1):
+                if k < len(steps):
+                    c, hf = steps[k]
+                    a_grouped[k] = work.tile([P, BANK, PACK], BF16, name="a_grouped", bufs=3, align_bytes=64)
+                    nc.vector.tensor_tensor(
+                        out=a_grouped[k][:],
+                        in0=scaled[c][:, :, hf * BANK : (hf + 1) * BANK].rearrange("p t i -> p i t"),
+                        in1=r_rows[hf][:].unsqueeze(2).to_broadcast([P, BANK, PACK]),
+                        op=ALU.mult,
+                    )
+                if k > 0:
+                    c, hf = steps[k - 1]
+                    cols = slice(hf * BANK, (hf + 1) * BANK)
+                    nc.vector.quantize_mx(
+                        out=a_codes[:, c, cols].bitcast(FP8X4),
+                        scales=a_scales[:, c, cols],
+                        in_=a_grouped[k - 1][:].rearrange("p i t -> p (i t)"),
+                    )
+
+            for st in range(BLOCKS // STORE_BLOCKS):
+                result = work.tile([P, STORE_BLOCKS, F_OUT], F32, name="result", bufs=3)
+                for k in range(STORE_BLOCKS):
+                    i_cols = slice((st * STORE_BLOCKS + k) * P, (st * STORE_BLOCKS + k + 1) * P)
+                    out_acc = psum.tile([P, F_OUT], F32, name="out_acc", tag="out_acc")
+                    for c in range(PASSES):
+                        nc.tensor.matmul_mx(
+                            out=out_acc[:],
+                            lhsT=a_codes[:, c, i_cols].bitcast(FP8X4),
+                            lhsT_scale=a_scales[:, c, i_cols],
+                            rhs=h_codes[:, c, :].bitcast(FP8X4),
+                            rhs_scale=h_scales[:, c, :],
+                            start=(c == 0),
+                            stop=(c == PASSES - 1),
+                        )
+                    nc.vector.tensor_tensor(out=result[:, k, :], in0=out_acc[:], in1=bias[:], op=ALU.add)
+                nc.scalar.activation(out=result[:], in_=result[:], func=ACT.Relu)
+                rows = out[g, st * STORE_BLOCKS * P : (st + 1) * STORE_BLOCKS * P, :]
+                nc.scalar.dma_start(out=rows.rearrange("(k m) f -> m k f", m=P), in_=result[:])

@@ -24,6 +24,7 @@ HALVES = NODES // BANK
 ONES_COLS = 32
 SCALAR_PLANES = 1
 STORE_BLOCKS = 2
+ACC_BANKS = 6
 
 FLOPS = 2 * GRAPHS * NODES * F_IN * F_OUT + 2 * GRAPHS * NODES * NODES * F_OUT
 
@@ -31,6 +32,7 @@ FLOPS = 2 * GRAPHS * NODES * F_IN * F_OUT + 2 * GRAPHS * NODES * NODES * F_OUT
 def tile_gcn_pa_kernel(tc, batch_graph, adj, W1, b1, out):
     nc = tc.nc
     with ExitStack() as ctx:
+        ctx.enter_context(tc.manual_schedule())
         consts = ctx.enter_context(tc.tile_pool(name="consts", bufs=1))
         inputs = ctx.enter_context(tc.tile_pool(name="inputs", bufs=GRAPHS))
         work = ctx.enter_context(tc.tile_pool(name="work", bufs=2))
@@ -58,10 +60,12 @@ def tile_gcn_pa_kernel(tc, batch_graph, adj, W1, b1, out):
             in_=W1.rearrange("(u q e) f -> q u (e f)", u=2, e=2),
         )
         load_x(0)
+        load_x(1)
         nc.sync.dma_start(out=bias_bf[:], in_=b1.partition_broadcast(P))
-        for g in range(1, GRAPHS):
-            load_adj(g)
+        load_adj(1)
+        for g in range(2, GRAPHS):
             load_x(g)
+            load_adj(g)
 
         warm = consts.tile([P, 1], F32, name="warm")
         nc.vector.memset(warm[:], 1.0)
@@ -81,151 +85,216 @@ def tile_gcn_pa_kernel(tc, batch_graph, adj, W1, b1, out):
             in_=w_grouped[:].rearrange("q f t -> q (f t)"),
         )
         bias = consts.tile([P, F_OUT], F32, name="bias")
-        nc.vector.tensor_copy(out=bias[:], in_=bias_bf[:])
 
-        for g in range(GRAPHS):
-            colsum = psum.tile([P, BLOCKS, ONES_COLS], F32, name="colsum", tag="plain")
+        colsum = {}
+        safe = {}
+        root = {}
+        r_col = {}
+        r_row = {}
+        x_grouped = {}
+        x_codes = {}
+        x_scales = {}
+        h_grouped = {}
+        h_codes = {}
+        h_scales = {}
+        planes = {}
+        a_grouped = {}
+        a_codes = {}
+        a_scales = {}
+
+        def column_sums(g):
+            colsum[g] = psum.tile([P, BLOCKS, ONES_COLS], F32, name="colsum", tag="acc", bufs=ACC_BANKS)
             for nb in range(BLOCKS):
                 for mb in range(BLOCKS):
                     nc.tensor.matmul(
-                        out=colsum[:, nb, :],
+                        out=colsum[g][:, nb, :],
                         lhsT=adj_sb[g][:, mb, nb * P : (nb + 1) * P],
                         rhs=ones[:],
                         start=(mb == 0),
                         stop=(mb == BLOCKS - 1),
                     )
-            sums = colsum[:, :, 0]
+
+        def r_start(g):
+            sums = colsum[g][:, :, 0]
             is_zero = work.tile([P, BLOCKS], F32, name="is_zero")
-            safe = work.tile([P, BLOCKS], F32, name="safe")
-            root = work.tile([P, BLOCKS], F32, name="root")
-            inv_root = work.tile([P, BLOCKS], F32, name="inv_root")
-            r_col = work.tile([P, BLOCKS], F32, name="r_col")
+            safe[g] = work.tile([P, BLOCKS], F32, name="safe")
+            root[g] = work.tile([P, BLOCKS], F32, name="root")
             nc.vector.tensor_single_scalar(out=is_zero[:], in_=sums, scalar=0.0, op=ALU.is_le)
-            nc.vector.tensor_tensor(out=safe[:], in0=sums, in1=is_zero[:], op=ALU.add)
-            nc.scalar.sqrt(out=root[:], in_=safe[:])
-            nc.vector.reciprocal(out=inv_root[:], in_=root[:])
+            nc.vector.tensor_tensor(out=safe[g][:], in0=sums, in1=is_zero[:], op=ALU.add)
+            nc.scalar.sqrt(out=root[g][:], in_=safe[g][:])
+
+        def r_finish(g):
+            inv_root = work.tile([P, BLOCKS], F32, name="inv_root")
+            r_col[g] = work.tile([P, BLOCKS], F32, name="r_col")
+            nc.vector.reciprocal(out=inv_root[:], in_=root[g][:])
             nc.vector.scalar_tensor_tensor(
-                out=r_col[:], in0=sums, scalar=0.0, in1=inv_root[:], op0=ALU.is_gt, op1=ALU.mult
+                out=r_col[g][:], in0=colsum[g][:, :, 0], scalar=0.0, in1=inv_root[:], op0=ALU.is_gt, op1=ALU.mult
             )
 
-            repeated = work.tile([P, BLOCKS, P], F32, name="repeated")
-            nc.gpsimd.tensor_scalar(
-                out=repeated[:],
-                in0=r_col[:].unsqueeze(2).to_broadcast([P, BLOCKS, P]),
-                scalar1=1.0,
-                scalar2=0.0,
-                op0=ALU.mult,
-                op1=ALU.add,
-            )
-            r_rows = []
+        def r_rows(g):
             for hf in range(HALVES):
-                r_row = psum.tile([P, BANK], F32, name="r_row", tag="r_row")
+                r_row[g, hf] = psum.tile([P, BANK], F32, name="r_row", tag="r_row")
                 for k in range(BANK // P):
-                    nc.tensor.transpose(r_row[:, k * P : (k + 1) * P], repeated[:, hf * (BANK // P) + k, :], ident[:])
-                r_rows.append(r_row)
-
-            x_codes = work.tile([P, NODES], U32, name="x_codes", align_bytes=64)
-            x_scales = work.tile([P, NODES], U8, name="x_scales", align_bytes=64)
-            for hf in range(HALVES):
-                x_grouped = work.tile([P, BANK * PACK], BF16, name="x_grouped", align_bytes=64)
-                x_words = x_grouped[:].bitcast(F32).rearrange("q (n u) -> q n u", u=2)
-                for pair in range(2):
-                    x_t = psum.tile([P, 2, 2, P], F32, name="x_t", tag="plain")
-                    for i in range(2):
-                        words = x_sb[g][:, 4 * hf + 2 * pair + i, :].bitcast(F32)
-                        for u in range(2):
-                            nc.tensor.transpose(x_t[:, i, u, :], words[:, u * P : (u + 1) * P], ident[:])
-                    nc.scalar.copy(
-                        out=x_words[:, pair * 2 * P : (pair + 1) * 2 * P, :].rearrange("q (i n) u -> q i n u", i=2),
-                        in_=x_t[:].rearrange("q i u n -> q i n u"),
+                    b = hf * (BANK // P) + k
+                    nc.tensor.matmul(
+                        out=r_row[g, hf][:, k * P : (k + 1) * P],
+                        lhsT=r_col[g][:, b : b + 1].to_broadcast([P, P]),
+                        rhs=ident[:],
+                        start=True,
+                        stop=True,
                     )
-                cols = slice(hf * BANK, (hf + 1) * BANK)
-                nc.vector.quantize_mx(out=x_codes[:, cols].bitcast(FP8X4), scales=x_scales[:, cols], in_=x_grouped[:])
 
-            h_codes = work.tile([P, PASSES, F_OUT], U32, name="h_codes", align_bytes=64)
-            h_scales = work.tile([P, PASSES, F_OUT], U8, name="h_scales", align_bytes=64)
-            for c in range(PASSES):
-                h_grouped = work.tile([P, F_OUT, PACK], BF16, name="h_grouped", align_bytes=64)
-                for fq in range(F_OUT // P):
-                    f_cols = slice(fq * P, (fq + 1) * P)
-                    h_acc = psum.tile([P, PACK, P], F32, name="h_acc", tag="h_acc")
-                    for t in range(PACK):
-                        n_cols = slice((c * PACK + t) * P, (c * PACK + t + 1) * P)
-                        nc.tensor.matmul_mx(
-                            out=h_acc[:, t, :],
-                            lhsT=x_codes[:, n_cols].bitcast(FP8X4),
-                            lhsT_scale=x_scales[:, n_cols],
-                            rhs=w_codes[:, f_cols].bitcast(FP8X4),
-                            rhs_scale=w_scales[:, f_cols],
-                            start=True,
-                            stop=True,
-                        )
-                    nc.scalar.copy(out=h_grouped[:, f_cols, :], in_=h_acc[:].rearrange("p t f -> p f t"))
-                nc.vector.quantize_mx(
-                    out=h_codes[:, c, :].bitcast(FP8X4),
-                    scales=h_scales[:, c, :],
-                    in_=h_grouped[:].rearrange("p f t -> p (f t)"),
+        def x_transpose(g, hf):
+            x_grouped[g, hf] = work.tile([P, BANK * PACK], BF16, name="x_grouped", align_bytes=64)
+            x_words = x_grouped[g, hf][:].bitcast(F32).rearrange("q (n u) -> q n u", u=2)
+            for pair in range(2):
+                x_t = psum.tile([P, 2, 2, P], F32, name="x_t", tag="acc", bufs=ACC_BANKS)
+                for i in range(2):
+                    words = x_sb[g][:, 4 * hf + 2 * pair + i, :].bitcast(F32)
+                    for u in range(2):
+                        nc.tensor.transpose(x_t[:, i, u, :], words[:, u * P : (u + 1) * P], ident[:])
+                nc.scalar.copy(
+                    out=x_words[:, pair * 2 * P : (pair + 1) * 2 * P, :].rearrange("q (i n) u -> q i n u", i=2),
+                    in_=x_t[:].rearrange("q i u n -> q i n u"),
                 )
 
-            a_codes = work.tile([P, PASSES, NODES], U32, name="a_codes", align_bytes=64)
-            a_scales = work.tile([P, PASSES, NODES], U8, name="a_scales", align_bytes=64)
-            scaled = []
-            for c in range(PASSES):
-                planes = work.tile([P, PACK, NODES], F32, name="planes")
+        def x_quantise(g, hf):
+            if hf == 0:
+                x_codes[g] = work.tile([P, NODES], U32, name="x_codes", align_bytes=64)
+                x_scales[g] = work.tile([P, NODES], U8, name="x_scales", align_bytes=64)
+            cols = slice(hf * BANK, (hf + 1) * BANK)
+            nc.vector.quantize_mx(
+                out=x_codes[g][:, cols].bitcast(FP8X4), scales=x_scales[g][:, cols], in_=x_grouped[g, hf][:]
+            )
+
+        def h_matmul(g, c):
+            h_grouped[g, c] = work.tile([P, F_OUT, PACK], BF16, name="h_grouped", align_bytes=64)
+            for fq in range(F_OUT // P):
+                f_cols = slice(fq * P, (fq + 1) * P)
+                h_acc = psum.tile([P, PACK, P], F32, name="h_acc", tag="acc", bufs=ACC_BANKS)
                 for t in range(PACK):
-                    b = c * PACK + t
-                    if t < SCALAR_PLANES:
-                        nc.scalar.activation(
-                            out=planes[:, t, :], in_=adj_sb[g][:, b, :], func=ACT.Copy, scale=r_col[:, b : b + 1]
-                        )
-                    else:
-                        nc.gpsimd.tensor_scalar(
-                            out=planes[:, t, :],
-                            in0=adj_sb[g][:, b, :],
-                            scalar1=r_col[:, b : b + 1],
-                            scalar2=0.0,
-                            op0=ALU.mult,
-                            op1=ALU.add,
-                        )
-                scaled.append(planes)
-
-            steps = [(c, hf) for c in range(PASSES) for hf in range(HALVES)]
-            a_grouped = {}
-            for k in range(len(steps) + 1):
-                if k < len(steps):
-                    c, hf = steps[k]
-                    a_grouped[k] = work.tile([P, BANK, PACK], BF16, name="a_grouped", bufs=3, align_bytes=64)
-                    nc.vector.tensor_tensor(
-                        out=a_grouped[k][:],
-                        in0=scaled[c][:, :, hf * BANK : (hf + 1) * BANK].rearrange("p t i -> p i t"),
-                        in1=r_rows[hf][:].unsqueeze(2).to_broadcast([P, BANK, PACK]),
-                        op=ALU.mult,
+                    n_cols = slice((c * PACK + t) * P, (c * PACK + t + 1) * P)
+                    nc.tensor.matmul_mx(
+                        out=h_acc[:, t, :],
+                        lhsT=x_codes[g][:, n_cols].bitcast(FP8X4),
+                        lhsT_scale=x_scales[g][:, n_cols],
+                        rhs=w_codes[:, f_cols].bitcast(FP8X4),
+                        rhs_scale=w_scales[:, f_cols],
+                        start=True,
+                        stop=True,
                     )
-                if k > 0:
-                    c, hf = steps[k - 1]
-                    cols = slice(hf * BANK, (hf + 1) * BANK)
-                    nc.vector.quantize_mx(
-                        out=a_codes[:, c, cols].bitcast(FP8X4),
-                        scales=a_scales[:, c, cols],
-                        in_=a_grouped[k - 1][:].rearrange("p i t -> p (i t)"),
+                nc.scalar.copy(out=h_grouped[g, c][:, f_cols, :], in_=h_acc[:].rearrange("p t f -> p f t"))
+
+        def h_quantise(g, c):
+            if c == 0:
+                h_codes[g] = work.tile([P, PASSES, F_OUT], U32, name="h_codes", align_bytes=64)
+                h_scales[g] = work.tile([P, PASSES, F_OUT], U8, name="h_scales", align_bytes=64)
+            nc.vector.quantize_mx(
+                out=h_codes[g][:, c, :].bitcast(FP8X4),
+                scales=h_scales[g][:, c, :],
+                in_=h_grouped[g, c][:].rearrange("p f t -> p (f t)"),
+            )
+
+        def scale_planes(g, c):
+            planes[g, c] = work.tile([P, PACK, NODES], F32, name="planes")
+            for t in range(PACK):
+                b = c * PACK + t
+                if t < SCALAR_PLANES:
+                    nc.scalar.activation(
+                        out=planes[g, c][:, t, :], in_=adj_sb[g][:, b, :], func=ACT.Copy, scale=r_col[g][:, b : b + 1]
+                    )
+                else:
+                    nc.gpsimd.tensor_scalar(
+                        out=planes[g, c][:, t, :],
+                        in0=adj_sb[g][:, b, :],
+                        scalar1=r_col[g][:, b : b + 1],
+                        scalar2=0.0,
+                        op0=ALU.mult,
+                        op1=ALU.add,
                     )
 
+        def a_multiply(g, c, hf):
+            a_grouped[g, c, hf] = work.tile([P, BANK, PACK], BF16, name="a_grouped", bufs=3, align_bytes=64)
+            nc.vector.tensor_tensor(
+                out=a_grouped[g, c, hf][:],
+                in0=planes[g, c][:, :, hf * BANK : (hf + 1) * BANK].rearrange("p t i -> p i t"),
+                in1=r_row[g, hf][:].unsqueeze(2).to_broadcast([P, BANK, PACK]),
+                op=ALU.mult,
+            )
+
+        def a_quantise(g, c, hf):
+            if (c, hf) == (0, 0):
+                a_codes[g] = work.tile([P, PASSES, NODES], U32, name="a_codes", align_bytes=64)
+                a_scales[g] = work.tile([P, PASSES, NODES], U8, name="a_scales", align_bytes=64)
+            cols = slice(hf * BANK, (hf + 1) * BANK)
+            nc.vector.quantize_mx(
+                out=a_codes[g][:, c, cols].bitcast(FP8X4),
+                scales=a_scales[g][:, c, cols],
+                in_=a_grouped[g, c, hf][:].rearrange("p i t -> p (i t)"),
+            )
+
+        def out_blocks(g, st):
+            result = work.tile([P, STORE_BLOCKS, F_OUT], F32, name="result", bufs=4)
+            for k in range(STORE_BLOCKS):
+                i_cols = slice((st * STORE_BLOCKS + k) * P, (st * STORE_BLOCKS + k + 1) * P)
+                out_acc = psum.tile([P, F_OUT], F32, name="out_acc", tag="acc", bufs=ACC_BANKS)
+                for c in range(PASSES):
+                    nc.tensor.matmul_mx(
+                        out=out_acc[:],
+                        lhsT=a_codes[g][:, c, i_cols].bitcast(FP8X4),
+                        lhsT_scale=a_scales[g][:, c, i_cols],
+                        rhs=h_codes[g][:, c, :].bitcast(FP8X4),
+                        rhs_scale=h_scales[g][:, c, :],
+                        start=(c == 0),
+                        stop=(c == PASSES - 1),
+                    )
+                nc.vector.tensor_tensor(out=result[:, k, :], in0=out_acc[:], in1=bias[:], op=ALU.add)
+            nc.scalar.activation(out=result[:], in_=result[:], func=ACT.Relu)
+            rows = out[g, st * STORE_BLOCKS * P : (st + 1) * STORE_BLOCKS * P, :]
+            nc.scalar.dma_start(out=rows.rearrange("(k m) f -> m k f", m=P), in_=result[:])
+
+        column_sums(0)
+        r_start(0)
+        r_finish(0)
+        scale_planes(0, 0)
+        r_rows(0)
+        x_transpose(0, 0)
+        x_transpose(0, 1)
+        scale_planes(0, 1)
+        x_quantise(0, 0)
+        x_quantise(0, 1)
+        h_matmul(0, 0)
+        h_matmul(0, 1)
+        nc.vector.tensor_copy(out=bias[:], in_=bias_bf[:])
+
+        for g in range(GRAPHS):
+            nxt = g + 1
+            more = nxt < GRAPHS
+            if more:
+                x_transpose(nxt, 0)
+                x_transpose(nxt, 1)
+                column_sums(nxt)
+            a_multiply(g, 0, 0)
+            a_multiply(g, 0, 1)
+            a_quantise(g, 0, 0)
+            if more:
+                x_quantise(nxt, 0)
+                x_quantise(nxt, 1)
+                r_start(nxt)
+                h_matmul(nxt, 0)
+            a_multiply(g, 1, 0)
+            a_quantise(g, 0, 1)
+            h_quantise(g, 0)
+            if more:
+                r_finish(nxt)
+                h_matmul(nxt, 1)
+                scale_planes(nxt, 0)
+            a_multiply(g, 1, 1)
+            a_quantise(g, 1, 0)
+            h_quantise(g, 1)
+            a_quantise(g, 1, 1)
+            if more:
+                r_rows(nxt)
+                scale_planes(nxt, 1)
             for st in range(BLOCKS // STORE_BLOCKS):
-                result = work.tile([P, STORE_BLOCKS, F_OUT], F32, name="result", bufs=3)
-                for k in range(STORE_BLOCKS):
-                    i_cols = slice((st * STORE_BLOCKS + k) * P, (st * STORE_BLOCKS + k + 1) * P)
-                    out_acc = psum.tile([P, F_OUT], F32, name="out_acc", tag="out_acc")
-                    for c in range(PASSES):
-                        nc.tensor.matmul_mx(
-                            out=out_acc[:],
-                            lhsT=a_codes[:, c, i_cols].bitcast(FP8X4),
-                            lhsT_scale=a_scales[:, c, i_cols],
-                            rhs=h_codes[:, c, :].bitcast(FP8X4),
-                            rhs_scale=h_scales[:, c, :],
-                            start=(c == 0),
-                            stop=(c == PASSES - 1),
-                        )
-                    nc.vector.tensor_tensor(out=result[:, k, :], in0=out_acc[:], in1=bias[:], op=ALU.add)
-                nc.scalar.activation(out=result[:], in_=result[:], func=ACT.Relu)
-                rows = out[g, st * STORE_BLOCKS * P : (st + 1) * STORE_BLOCKS * P, :]
-                nc.scalar.dma_start(out=rows.rearrange("(k m) f -> m k f", m=P), in_=result[:])
+                out_blocks(g, st)

@@ -24,6 +24,7 @@ HALVES = NODES // BANK
 ONES_COLS = 32
 SCALAR_PLANES = 1
 STORE_BLOCKS = 2
+ADJ_BUFS = 3
 ACC_BANKS = 6
 
 FLOPS = 2 * GRAPHS * NODES * F_IN * F_OUT + 2 * GRAPHS * NODES * NODES * F_OUT
@@ -38,12 +39,13 @@ def tile_gcn_pa_kernel(tc, batch_graph, adj, W1, b1, out):
         work = ctx.enter_context(tc.tile_pool(name="work", bufs=2))
         psum = ctx.enter_context(tc.psum_pool(name="psum", bufs=2))
 
-        adj_sb = [inputs.tile([P, BLOCKS, NODES], BF16, name="adj_sb", tag="adj_sb") for g in range(GRAPHS)]
+        adj_sb = {}
         x_sb = [inputs.tile([P, BLOCKS, F_IN], BF16, name="x_sb", tag="x_sb") for g in range(GRAPHS)]
         w_sb = consts.tile([P, PACK, F_OUT], BF16, name="w_sb")
         bias_bf = consts.tile([P, F_OUT], BF16, name="bias_bf")
 
         def load_adj(g):
+            adj_sb[g] = inputs.tile([P, BLOCKS, NODES], BF16, name="adj_sb", tag="adj_sb", bufs=ADJ_BUFS)
             for c in range(PASSES):
                 rows = adj[g, c * P * PACK : (c + 1) * P * PACK, :]
                 nc.sync.dma_start(
@@ -63,9 +65,9 @@ def tile_gcn_pa_kernel(tc, batch_graph, adj, W1, b1, out):
         load_x(1)
         nc.sync.dma_start(out=bias_bf[:], in_=b1.partition_broadcast(P))
         load_adj(1)
-        for g in range(2, GRAPHS):
-            load_x(g)
-            load_adj(g)
+        load_x(2)
+        load_adj(2)
+        load_x(3)
 
         warm = consts.tile([P, 1], F32, name="warm")
         nc.vector.memset(warm[:], 1.0)
@@ -101,6 +103,7 @@ def tile_gcn_pa_kernel(tc, batch_graph, adj, W1, b1, out):
         a_grouped = {}
         a_codes = {}
         a_scales = {}
+        out_acc = {}
 
         def column_sums(g):
             colsum[g] = psum.tile([P, BLOCKS, ONES_COLS], F32, name="colsum", tag="acc", bufs=ACC_BANKS)
@@ -196,7 +199,7 @@ def tile_gcn_pa_kernel(tc, batch_graph, adj, W1, b1, out):
             )
 
         def scale_planes(g, c):
-            planes[g, c] = work.tile([P, PACK, NODES], F32, name="planes")
+            planes[g, c] = work.tile([P, PACK, NODES], F32, name="planes", bufs=3)
             for t in range(PACK):
                 b = c * PACK + t
                 if t < SCALAR_PLANES:
@@ -233,14 +236,13 @@ def tile_gcn_pa_kernel(tc, batch_graph, adj, W1, b1, out):
                 in_=a_grouped[g, c, hf][:].rearrange("p i t -> p (i t)"),
             )
 
-        def out_blocks(g, st):
-            result = work.tile([P, STORE_BLOCKS, F_OUT], F32, name="result", bufs=4)
+        def out_matmul(g, st):
             for k in range(STORE_BLOCKS):
                 i_cols = slice((st * STORE_BLOCKS + k) * P, (st * STORE_BLOCKS + k + 1) * P)
-                out_acc = psum.tile([P, F_OUT], F32, name="out_acc", tag="acc", bufs=ACC_BANKS)
+                out_acc[g, st, k] = psum.tile([P, F_OUT], F32, name="out_acc", tag="acc", bufs=ACC_BANKS)
                 for c in range(PASSES):
                     nc.tensor.matmul_mx(
-                        out=out_acc[:],
+                        out=out_acc[g, st, k][:],
                         lhsT=a_codes[g][:, c, i_cols].bitcast(FP8X4),
                         lhsT_scale=a_scales[g][:, c, i_cols],
                         rhs=h_codes[g][:, c, :].bitcast(FP8X4),
@@ -248,53 +250,70 @@ def tile_gcn_pa_kernel(tc, batch_graph, adj, W1, b1, out):
                         start=(c == 0),
                         stop=(c == PASSES - 1),
                     )
-                nc.vector.tensor_tensor(out=result[:, k, :], in0=out_acc[:], in1=bias[:], op=ALU.add)
+
+        def out_finish(g, st):
+            result = work.tile([P, STORE_BLOCKS, F_OUT], F32, name="result", bufs=4)
+            for k in range(STORE_BLOCKS):
+                nc.vector.tensor_tensor(out=result[:, k, :], in0=out_acc[g, st, k][:], in1=bias[:], op=ALU.add)
             nc.scalar.activation(out=result[:], in_=result[:], func=ACT.Relu)
             rows = out[g, st * STORE_BLOCKS * P : (st + 1) * STORE_BLOCKS * P, :]
             nc.scalar.dma_start(out=rows.rearrange("(k m) f -> m k f", m=P), in_=result[:])
 
         column_sums(0)
         r_start(0)
+        x_transpose(0, 0)
+        x_transpose(0, 1)
         r_finish(0)
         scale_planes(0, 0)
         r_rows(0)
-        x_transpose(0, 0)
-        x_transpose(0, 1)
         scale_planes(0, 1)
+        load_adj(3)
         x_quantise(0, 0)
         x_quantise(0, 1)
+        nc.vector.tensor_copy(out=bias[:], in_=bias_bf[:])
+        x_transpose(1, 0)
+        x_transpose(1, 1)
+        column_sums(1)
         h_matmul(0, 0)
         h_matmul(0, 1)
-        nc.vector.tensor_copy(out=bias[:], in_=bias_bf[:])
 
         for g in range(GRAPHS):
             nxt = g + 1
             more = nxt < GRAPHS
-            if more:
-                x_transpose(nxt, 0)
-                x_transpose(nxt, 1)
-                column_sums(nxt)
+            more2 = nxt + 1 < GRAPHS
             a_multiply(g, 0, 0)
-            a_multiply(g, 0, 1)
-            a_quantise(g, 0, 0)
             if more:
                 x_quantise(nxt, 0)
                 x_quantise(nxt, 1)
                 r_start(nxt)
                 h_matmul(nxt, 0)
+                h_matmul(nxt, 1)
             a_multiply(g, 1, 0)
-            a_quantise(g, 0, 1)
-            h_quantise(g, 0)
             if more:
                 r_finish(nxt)
-                h_matmul(nxt, 1)
                 scale_planes(nxt, 0)
-            a_multiply(g, 1, 1)
+            a_quantise(g, 0, 0)
             a_quantise(g, 1, 0)
+            h_quantise(g, 0)
             h_quantise(g, 1)
+            out_matmul(g, 0)
+            out_matmul(g, 1)
+            if more2:
+                x_transpose(nxt + 1, 0)
+                x_transpose(nxt + 1, 1)
+            a_multiply(g, 0, 1)
+            if more:
+                scale_planes(nxt, 1)
+            a_multiply(g, 1, 1)
+            a_quantise(g, 0, 1)
             a_quantise(g, 1, 1)
+            out_matmul(g, 2)
+            out_finish(g, 0)
+            out_matmul(g, 3)
+            out_finish(g, 1)
             if more:
                 r_rows(nxt)
-                scale_planes(nxt, 1)
-            for st in range(BLOCKS // STORE_BLOCKS):
-                out_blocks(g, st)
+            if more2:
+                column_sums(nxt + 1)
+            out_finish(g, 2)
+            out_finish(g, 3)

@@ -22,7 +22,7 @@ PASSES = NODES // (P * PACK)
 BANK = 512
 HALVES = NODES // BANK
 ONES_COLS = 32
-SCALAR_PLANES = 1
+SCALAR_PLANES = 2
 STORE_BLOCKS = 2
 ADJ_BUFS = 3
 ACC_BANKS = 6

@@ -24,6 +24,7 @@ HALVES = NODES // BANK
 ONES_COLS = 32
 SCALAR_PLANES = 2
 STORE_BLOCKS = 2
+RUN = 4
 ADJ_BUFS = 3
 ACC_BANKS = 6
 
@@ -219,9 +220,12 @@ def tile_gcn_pa_kernel(tc, batch_graph, adj, W1, b1, out):
         def a_multiply(g, c, hf):
             a_grouped[g, c, hf] = work.tile([P, BANK, PACK], BF16, name="a_grouped", bufs=3, align_bytes=64)
             nc.vector.tensor_tensor(
-                out=a_grouped[g, c, hf][:],
-                in0=planes[g, c][:, :, hf * BANK : (hf + 1) * BANK].rearrange("p t i -> p i t"),
-                in1=r_row[g, hf][:].unsqueeze(2).to_broadcast([P, BANK, PACK]),
+                out=a_grouped[g, c, hf][:].rearrange("p (n i) t -> p n t i", i=RUN),
+                in0=planes[g, c][:, :, hf * BANK : (hf + 1) * BANK].rearrange("p t (n i) -> p n t i", i=RUN),
+                in1=r_row[g, hf][:]
+                .rearrange("p (n i) -> p n i", i=RUN)
+                .unsqueeze(2)
+                .to_broadcast([P, BANK // RUN, PACK, RUN]),
                 op=ALU.mult,
             )
 

@@ -25,7 +25,8 @@ ONES_COLS = 32
 SCALAR_PLANES = 2
 STORE_BLOCKS = 2
 RUN = 4
-ADJ_BUFS = 3
+GPSIMD_HALF = 0
+INPUT_BUFS = 3
 ACC_BANKS = 6
 
 FLOPS = 2 * GRAPHS * NODES * F_IN * F_OUT + 2 * GRAPHS * NODES * NODES * F_OUT
@@ -36,17 +37,17 @@ def tile_gcn_pa_kernel(tc, batch_graph, adj, W1, b1, out):
     with ExitStack() as ctx:
         ctx.enter_context(tc.manual_schedule())
         consts = ctx.enter_context(tc.tile_pool(name="consts", bufs=1))
-        inputs = ctx.enter_context(tc.tile_pool(name="inputs", bufs=GRAPHS))
+        inputs = ctx.enter_context(tc.tile_pool(name="inputs", bufs=INPUT_BUFS))
         work = ctx.enter_context(tc.tile_pool(name="work", bufs=2))
         psum = ctx.enter_context(tc.psum_pool(name="psum", bufs=2))
 
         adj_sb = {}
-        x_sb = [inputs.tile([P, BLOCKS, F_IN], BF16, name="x_sb", tag="x_sb") for g in range(GRAPHS)]
+        x_sb = {}
         w_sb = consts.tile([P, PACK, F_OUT], BF16, name="w_sb")
         bias_bf = consts.tile([P, F_OUT], BF16, name="bias_bf")
 
         def load_adj(g):
-            adj_sb[g] = inputs.tile([P, BLOCKS, NODES], BF16, name="adj_sb", tag="adj_sb", bufs=ADJ_BUFS)
+            adj_sb[g] = inputs.tile([P, BLOCKS, NODES], BF16, name="adj_sb", tag="adj_sb", bufs=INPUT_BUFS)
             for c in range(PASSES):
                 rows = adj[g, c * P * PACK : (c + 1) * P * PACK, :]
                 nc.sync.dma_start(
@@ -55,6 +56,7 @@ def tile_gcn_pa_kernel(tc, batch_graph, adj, W1, b1, out):
                 )
 
         def load_x(g):
+            x_sb[g] = inputs.tile([P, BLOCKS, F_IN], BF16, name="x_sb", tag="x_sb", bufs=INPUT_BUFS)
             nc.sync.dma_start(out=x_sb[g][:], in_=batch_graph[g].rearrange("(b p) k -> p b k", p=P))
 
         load_adj(0)
@@ -68,7 +70,6 @@ def tile_gcn_pa_kernel(tc, batch_graph, adj, W1, b1, out):
         load_adj(1)
         load_x(2)
         load_adj(2)
-        load_x(3)
 
         warm = consts.tile([P, 1], F32, name="warm")
         nc.vector.memset(warm[:], 1.0)
@@ -94,6 +95,7 @@ def tile_gcn_pa_kernel(tc, batch_graph, adj, W1, b1, out):
         root = {}
         r_col = {}
         r_row = {}
+        r_row_sb = {}
         x_grouped = {}
         x_codes = {}
         x_scales = {}
@@ -135,18 +137,20 @@ def tile_gcn_pa_kernel(tc, batch_graph, adj, W1, b1, out):
                 out=r_col[g][:], in0=colsum[g][:, :, 0], scalar=0.0, in1=inv_root[:], op0=ALU.is_gt, op1=ALU.mult
             )
 
-        def r_rows(g):
-            for hf in range(HALVES):
-                r_row[g, hf] = psum.tile([P, BANK], F32, name="r_row", tag="r_row")
-                for k in range(BANK // P):
-                    b = hf * (BANK // P) + k
-                    nc.tensor.matmul(
-                        out=r_row[g, hf][:, k * P : (k + 1) * P],
-                        lhsT=r_col[g][:, b : b + 1].to_broadcast([P, P]),
-                        rhs=ident[:],
-                        start=True,
-                        stop=True,
-                    )
+        def r_rows(g, hf):
+            r_row[g, hf] = psum.tile([P, BANK], F32, name="r_row", tag="r_row%d" % hf, bufs=1)
+            for k in range(BANK // P):
+                b = hf * (BANK // P) + k
+                nc.tensor.matmul(
+                    out=r_row[g, hf][:, k * P : (k + 1) * P],
+                    lhsT=r_col[g][:, b : b + 1].to_broadcast([P, P]),
+                    rhs=ident[:],
+                    start=True,
+                    stop=True,
+                )
+            if hf == GPSIMD_HALF:
+                r_row_sb[g] = work.tile([P, BANK], F32, name="r_row_sb")
+                nc.scalar.copy(out=r_row_sb[g][:], in_=r_row[g, hf][:])
 
         def x_transpose(g, hf):
             x_grouped[g, hf] = work.tile([P, BANK * PACK], BF16, name="x_grouped", align_bytes=64)
@@ -172,7 +176,7 @@ def tile_gcn_pa_kernel(tc, batch_graph, adj, W1, b1, out):
             )
 
         def h_matmul(g, c):
-            h_grouped[g, c] = work.tile([P, F_OUT, PACK], BF16, name="h_grouped", align_bytes=64)
+            h_grouped[g, c] = work.tile([P, F_OUT, PACK], BF16, name="h_grouped", bufs=2 * PASSES, align_bytes=64)
             for fq in range(F_OUT // P):
                 f_cols = slice(fq * P, (fq + 1) * P)
                 h_acc = psum.tile([P, PACK, P], F32, name="h_acc", tag="acc", bufs=ACC_BANKS)
@@ -218,7 +222,7 @@ def tile_gcn_pa_kernel(tc, batch_graph, adj, W1, b1, out):
                     )
 
         def a_multiply(g, c, hf):
-            a_grouped[g, c, hf] = work.tile([P, BANK, PACK], BF16, name="a_grouped", bufs=3, align_bytes=64)
+            a_grouped[g, c, hf] = work.tile([P, BANK, PACK], BF16, name="a_grouped", bufs=2, align_bytes=64)
             nc.vector.tensor_tensor(
                 out=a_grouped[g, c, hf][:].rearrange("p (n i) t -> p n t i", i=RUN),
                 in0=planes[g, c][:, :, hf * BANK : (hf + 1) * BANK].rearrange("p t (n i) -> p n t i", i=RUN),
@@ -226,6 +230,16 @@ def tile_gcn_pa_kernel(tc, batch_graph, adj, W1, b1, out):
                 .rearrange("p (n i) -> p n i", i=RUN)
                 .unsqueeze(2)
                 .to_broadcast([P, BANK // RUN, PACK, RUN]),
+                op=ALU.mult,
+            )
+
+        def a_multiply_gpsimd(g):
+            c, hf = PASSES - 1, GPSIMD_HALF
+            a_grouped[g, c, hf] = work.tile([P, BANK, PACK], BF16, name="a_grouped_gp", bufs=1, align_bytes=64)
+            nc.gpsimd.tensor_tensor(
+                out=a_grouped[g, c, hf][:],
+                in0=planes[g, c][:, :, hf * BANK : (hf + 1) * BANK].rearrange("p t i -> p i t"),
+                in1=r_row_sb[g][:].unsqueeze(2).to_broadcast([P, BANK, PACK]),
                 op=ALU.mult,
             )
 
@@ -269,8 +283,11 @@ def tile_gcn_pa_kernel(tc, batch_graph, adj, W1, b1, out):
         x_transpose(0, 1)
         r_finish(0)
         scale_planes(0, 0)
-        r_rows(0)
+        r_rows(0, 0)
+        r_rows(0, 1)
         scale_planes(0, 1)
+        a_multiply_gpsimd(0)
+        load_x(3)
         load_adj(3)
         x_quantise(0, 0)
         x_quantise(0, 1)
@@ -292,10 +309,12 @@ def tile_gcn_pa_kernel(tc, batch_graph, adj, W1, b1, out):
                 r_start(nxt)
                 h_matmul(nxt, 0)
                 h_matmul(nxt, 1)
-            a_multiply(g, 1, 0)
+            a_multiply(g, 0, 1)
             if more:
                 r_finish(nxt)
                 scale_planes(nxt, 0)
+                r_rows(nxt, 0)
+                scale_planes(nxt, 1)
             a_quantise(g, 0, 0)
             a_quantise(g, 1, 0)
             h_quantise(g, 0)
@@ -305,9 +324,6 @@ def tile_gcn_pa_kernel(tc, batch_graph, adj, W1, b1, out):
             if more2:
                 x_transpose(nxt + 1, 0)
                 x_transpose(nxt + 1, 1)
-            a_multiply(g, 0, 1)
-            if more:
-                scale_planes(nxt, 1)
             a_multiply(g, 1, 1)
             a_quantise(g, 0, 1)
             a_quantise(g, 1, 1)
@@ -316,7 +332,8 @@ def tile_gcn_pa_kernel(tc, batch_graph, adj, W1, b1, out):
             out_matmul(g, 3)
             out_finish(g, 1)
             if more:
-                r_rows(nxt)
+                a_multiply_gpsimd(nxt)
+                r_rows(nxt, 1)
             if more2:
                 column_sums(nxt + 1)
             out_finish(g, 2)

@@ -10,6 +10,7 @@ U8 = mybir.dt.uint8
 FP8X4 = mybir.dt.float8_e4m3fn_x4
 ALU = mybir.AluOpType
 ACT = mybir.ActivationFunctionType
+AXIS = mybir.AxisListType
 
 P = 128
 PACK = 4
@@ -91,7 +92,7 @@ def tile_gcn_pa_kernel(tc, batch_graph, adj, W1, b1, out):
         bias = consts.tile([P, F_OUT], F32, name="bias")
 
         colsum = {}
-        safe = {}
+        sums = {}
         root = {}
         r_col = {}
         r_row = {}
@@ -109,32 +110,36 @@ def tile_gcn_pa_kernel(tc, batch_graph, adj, W1, b1, out):
         out_acc = {}
 
         def column_sums(g):
-            colsum[g] = psum.tile([P, BLOCKS, ONES_COLS], F32, name="colsum", tag="acc", bufs=ACC_BANKS)
-            for nb in range(BLOCKS):
-                for mb in range(BLOCKS):
-                    nc.tensor.matmul(
-                        out=colsum[g][:, nb, :],
-                        lhsT=adj_sb[g][:, mb, nb * P : (nb + 1) * P],
-                        rhs=ones[:],
-                        start=(mb == 0),
-                        stop=(mb == BLOCKS - 1),
-                    )
+            colsum[g] = psum.tile([P, PASSES, BLOCKS, ONES_COLS], F32, name="colsum", tag="acc", bufs=ACC_BANKS)
+            for c in range(PASSES):
+                for nb in range(BLOCKS):
+                    for t in range(PACK):
+                        nc.tensor.matmul(
+                            out=colsum[g][:, c, nb, :],
+                            lhsT=adj_sb[g][:, c * PACK + t, nb * P : (nb + 1) * P],
+                            rhs=ones[:],
+                            start=(t == 0),
+                            stop=(t == PACK - 1),
+                        )
 
         def r_start(g):
-            sums = colsum[g][:, :, 0]
+            sums[g] = work.tile([P, BLOCKS], F32, name="sums")
             is_zero = work.tile([P, BLOCKS], F32, name="is_zero")
-            safe[g] = work.tile([P, BLOCKS], F32, name="safe")
+            safe = work.tile([P, BLOCKS], F32, name="safe")
             root[g] = work.tile([P, BLOCKS], F32, name="root")
-            nc.vector.tensor_single_scalar(out=is_zero[:], in_=sums, scalar=0.0, op=ALU.is_le)
-            nc.vector.tensor_tensor(out=safe[g][:], in0=sums, in1=is_zero[:], op=ALU.add)
-            nc.scalar.sqrt(out=root[g][:], in_=safe[g][:])
+            nc.vector.tensor_reduce(
+                out=sums[g][:], in_=colsum[g][:, :, :, 0].rearrange("p c b -> p b c"), axis=AXIS.X, op=ALU.add
+            )
+            nc.vector.tensor_single_scalar(out=is_zero[:], in_=sums[g][:], scalar=0.0, op=ALU.is_le)
+            nc.vector.tensor_tensor(out=safe[:], in0=sums[g][:], in1=is_zero[:], op=ALU.add)
+            nc.scalar.sqrt(out=root[g][:], in_=safe[:])
 
         def r_finish(g):
             inv_root = work.tile([P, BLOCKS], F32, name="inv_root")
             r_col[g] = work.tile([P, BLOCKS], F32, name="r_col")
             nc.vector.reciprocal(out=inv_root[:], in_=root[g][:])
             nc.vector.scalar_tensor_tensor(
-                out=r_col[g][:], in0=colsum[g][:, :, 0], scalar=0.0, in1=inv_root[:], op0=ALU.is_gt, op1=ALU.mult
+                out=r_col[g][:], in0=sums[g][:], scalar=0.0, in1=inv_root[:], op0=ALU.is_gt, op1=ALU.mult
             )
 
         def r_rows(g, hf):
@@ -152,13 +157,13 @@ def tile_gcn_pa_kernel(tc, batch_graph, adj, W1, b1, out):
                 r_row_sb[g] = work.tile([P, BANK], F32, name="r_row_sb")
                 nc.scalar.copy(out=r_row_sb[g][:], in_=r_row[g, hf][:])
 
-        def x_transpose(g, hf):
-            x_grouped[g, hf] = work.tile([P, BANK * PACK], BF16, name="x_grouped", align_bytes=64)
-            x_words = x_grouped[g, hf][:].bitcast(F32).rearrange("q (n u) -> q n u", u=2)
-            for pair in range(2):
+        def x_transpose(g):
+            x_grouped[g] = work.tile([P, NODES * PACK], BF16, name="x_grouped", bufs=1, align_bytes=64)
+            x_words = x_grouped[g][:].bitcast(F32).rearrange("q (n u) -> q n u", u=2)
+            for pair in range(BLOCKS // 2):
                 x_t = psum.tile([P, 2, 2, P], F32, name="x_t", tag="acc", bufs=ACC_BANKS)
                 for i in range(2):
-                    words = x_sb[g][:, 4 * hf + 2 * pair + i, :].bitcast(F32)
+                    words = x_sb[g][:, 2 * pair + i, :].bitcast(F32)
                     for u in range(2):
                         nc.tensor.transpose(x_t[:, i, u, :], words[:, u * P : (u + 1) * P], ident[:])
                 nc.scalar.copy(
@@ -166,17 +171,14 @@ def tile_gcn_pa_kernel(tc, batch_graph, adj, W1, b1, out):
                     in_=x_t[:].rearrange("q i u n -> q i n u"),
                 )
 
-        def x_quantise(g, hf):
-            if hf == 0:
-                x_codes[g] = work.tile([P, NODES], U32, name="x_codes", align_bytes=64)
-                x_scales[g] = work.tile([P, NODES], U8, name="x_scales", align_bytes=64)
-            cols = slice(hf * BANK, (hf + 1) * BANK)
-            nc.vector.quantize_mx(
-                out=x_codes[g][:, cols].bitcast(FP8X4), scales=x_scales[g][:, cols], in_=x_grouped[g, hf][:]
-            )
+        def x_quantise(g):
+            x_codes[g] = work.tile([P, NODES], U32, name="x_codes", align_bytes=64)
+            x_scales[g] = work.tile([P, NODES], U8, name="x_scales", align_bytes=64)
+            nc.vector.quantize_mx(out=x_codes[g][:].bitcast(FP8X4), scales=x_scales[g][:], in_=x_grouped[g][:])
 
         def h_matmul(g, c):
-            h_grouped[g, c] = work.tile([P, F_OUT, PACK], BF16, name="h_grouped", bufs=2 * PASSES, align_bytes=64)
+            if c == 0:
+                h_grouped[g] = work.tile([P, PASSES, F_OUT, PACK], BF16, name="h_grouped", align_bytes=64)
             for fq in range(F_OUT // P):
                 f_cols = slice(fq * P, (fq + 1) * P)
                 h_acc = psum.tile([P, PACK, P], F32, name="h_acc", tag="acc", bufs=ACC_BANKS)
@@ -191,16 +193,15 @@ def tile_gcn_pa_kernel(tc, batch_graph, adj, W1, b1, out):
                         start=True,
                         stop=True,
                     )
-                nc.scalar.copy(out=h_grouped[g, c][:, f_cols, :], in_=h_acc[:].rearrange("p t f -> p f t"))
+                nc.scalar.copy(out=h_grouped[g][:, c, f_cols, :], in_=h_acc[:].rearrange("p t f -> p f t"))
 
-        def h_quantise(g, c):
-            if c == 0:
-                h_codes[g] = work.tile([P, PASSES, F_OUT], U32, name="h_codes", align_bytes=64)
-                h_scales[g] = work.tile([P, PASSES, F_OUT], U8, name="h_scales", align_bytes=64)
+        def h_quantise(g):
+            h_codes[g] = work.tile([P, PASSES, F_OUT], U32, name="h_codes", align_bytes=64)
+            h_scales[g] = work.tile([P, PASSES, F_OUT], U8, name="h_scales", align_bytes=64)
             nc.vector.quantize_mx(
-                out=h_codes[g][:, c, :].bitcast(FP8X4),
-                scales=h_scales[g][:, c, :],
-                in_=h_grouped[g, c][:].rearrange("p f t -> p (f t)"),
+                out=h_codes[g][:].rearrange("p c f -> p (c f)").bitcast(FP8X4),
+                scales=h_scales[g][:].rearrange("p c f -> p (c f)"),
+                in_=h_grouped[g][:].rearrange("p c f t -> p (c f t)"),
             )
 
         def scale_planes(g, c):
@@ -275,12 +276,11 @@ def tile_gcn_pa_kernel(tc, batch_graph, adj, W1, b1, out):
                 nc.vector.tensor_tensor(out=result[:, k, :], in0=out_acc[g, st, k][:], in1=bias[:], op=ALU.add)
             nc.scalar.activation(out=result[:], in_=result[:], func=ACT.Relu)
             rows = out[g, st * STORE_BLOCKS * P : (st + 1) * STORE_BLOCKS * P, :]
-            nc.scalar.dma_start(out=rows.rearrange("(k m) f -> m k f", m=P), in_=result[:])
+            nc.sync.dma_start(out=rows.rearrange("(k m) f -> m k f", m=P), in_=result[:])
 
         column_sums(0)
         r_start(0)
-        x_transpose(0, 0)
-        x_transpose(0, 1)
+        x_transpose(0)
         r_finish(0)
         scale_planes(0, 0)
         r_rows(0, 0)
@@ -289,11 +289,9 @@ def tile_gcn_pa_kernel(tc, batch_graph, adj, W1, b1, out):
         a_multiply_gpsimd(0)
         load_x(3)
         load_adj(3)
-        x_quantise(0, 0)
-        x_quantise(0, 1)
+        x_quantise(0)
         nc.vector.tensor_copy(out=bias[:], in_=bias_bf[:])
-        x_transpose(1, 0)
-        x_transpose(1, 1)
+        x_transpose(1)
         column_sums(1)
         h_matmul(0, 0)
         h_matmul(0, 1)
@@ -304,8 +302,7 @@ def tile_gcn_pa_kernel(tc, batch_graph, adj, W1, b1, out):
             more2 = nxt + 1 < GRAPHS
             a_multiply(g, 0, 0)
             if more:
-                x_quantise(nxt, 0)
-                x_quantise(nxt, 1)
+                x_quantise(nxt)
                 r_start(nxt)
                 h_matmul(nxt, 0)
                 h_matmul(nxt, 1)
@@ -317,13 +314,11 @@ def tile_gcn_pa_kernel(tc, batch_graph, adj, W1, b1, out):
                 scale_planes(nxt, 1)
             a_quantise(g, 0, 0)
             a_quantise(g, 1, 0)
-            h_quantise(g, 0)
-            h_quantise(g, 1)
+            h_quantise(g)
             out_matmul(g, 0)
             out_matmul(g, 1)
             if more2:
-                x_transpose(nxt + 1, 0)
-                x_transpose(nxt + 1, 1)
+                x_transpose(nxt + 1)
             a_multiply(g, 1, 1)
             a_quantise(g, 0, 1)
             a_quantise(g, 1, 1)

@@ -273,10 +273,10 @@ def tile_gcn_pa_kernel(tc, batch_graph, adj, W1, b1, out):
         def out_finish(g, st):
             result = work.tile([P, STORE_BLOCKS, F_OUT], F32, name="result", bufs=4)
             for k in range(STORE_BLOCKS):
+                block = st * STORE_BLOCKS + k
                 nc.vector.tensor_tensor(out=result[:, k, :], in0=out_acc[g, st, k][:], in1=bias[:], op=ALU.add)
-            nc.scalar.activation(out=result[:], in_=result[:], func=ACT.Relu)
-            rows = out[g, st * STORE_BLOCKS * P : (st + 1) * STORE_BLOCKS * P, :]
-            nc.sync.dma_start(out=rows.rearrange("(k m) f -> m k f", m=P), in_=result[:])
+                nc.scalar.activation(out=result[:, k, :], in_=result[:, k, :], func=ACT.Relu)
+                nc.sync.dma_start(out=out[g, block * P : (block + 1) * P, :], in_=result[:, k, :])
 
         column_sums(0)
         r_start(0)
@@ -317,14 +317,14 @@ def tile_gcn_pa_kernel(tc, batch_graph, adj, W1, b1, out):
             h_quantise(g)
             out_matmul(g, 0)
             out_matmul(g, 1)
-            if more2:
-                x_transpose(nxt + 1)
             a_multiply(g, 1, 1)
             a_quantise(g, 0, 1)
             a_quantise(g, 1, 1)
             out_matmul(g, 2)
             out_finish(g, 0)
             out_matmul(g, 3)
+            if more2:
+                x_transpose(nxt + 1)
             out_finish(g, 1)
             if more:
                 a_multiply_gpsimd(nxt)

@@ -23,10 +23,12 @@ PASSES = NODES // (P * PACK)
 BANK = 512
 HALVES = NODES // BANK
 ONES_COLS = 32
-SCALAR_PLANES = 2
-STORE_BLOCKS = 2
+TINY = 2.0**-126
 RUN = 4
-GPSIMD_HALF = 0
+GP_PARTS = 4
+GPSIMD_HALF = 1
+PAIRS = BLOCKS // 2
+FQ = F_OUT // P
 INPUT_BUFS = 3
 ACC_BANKS = 6
 
@@ -36,7 +38,7 @@ FLOPS = 2 * GRAPHS * NODES * F_IN * F_OUT + 2 * GRAPHS * NODES * NODES * F_OUT
 def tile_gcn_pa_kernel(tc, batch_graph, adj, W1, b1, out):
     nc = tc.nc
     with ExitStack() as ctx:
-        ctx.enter_context(tc.manual_schedule())
+        ctx.enter_context(tc.manual_schedule(engines={mybir.EngineType.SP}))
         consts = ctx.enter_context(tc.tile_pool(name="consts", bufs=1))
         inputs = ctx.enter_context(tc.tile_pool(name="inputs", bufs=INPUT_BUFS))
         work = ctx.enter_context(tc.tile_pool(name="work", bufs=2))
@@ -57,24 +59,29 @@ def tile_gcn_pa_kernel(tc, batch_graph, adj, W1, b1, out):
                 )
 
         def load_x(g):
-            x_sb[g] = inputs.tile([P, BLOCKS, F_IN], BF16, name="x_sb", tag="x_sb", bufs=INPUT_BUFS)
-            nc.sync.dma_start(out=x_sb[g][:], in_=batch_graph[g].rearrange("(b p) k -> p b k", p=P))
+            x_sb[g] = inputs.tile([P, BLOCKS, F_IN], BF16, name="x_sb", tag="x_sb", bufs=2)
+            half = BLOCKS // 2
+            for k in range(2):
+                rows = batch_graph[g, k * half * P : (k + 1) * half * P, :]
+                nc.sync.dma_start(
+                    out=x_sb[g][:, k * half : (k + 1) * half, :], in_=rows.rearrange("(b p) k -> p b k", p=P)
+                )
 
-        load_adj(0)
         nc.sync.dma_start(
             out=w_sb[:].rearrange("q (u e) f -> q u (e f)", u=2),
             in_=W1.rearrange("(u q e) f -> q u (e f)", u=2, e=2),
         )
         load_x(0)
+        load_adj(0)
         load_x(1)
         nc.sync.dma_start(out=bias_bf[:], in_=b1.partition_broadcast(P))
         load_adj(1)
-        load_x(2)
-        load_adj(2)
 
         warm = consts.tile([P, 1], F32, name="warm")
         nc.vector.memset(warm[:], 1.0)
         nc.scalar.sqrt(out=warm[:], in_=warm[:])
+        tiny = consts.tile([P, 1], F32, name="tiny")
+        nc.vector.memset(tiny[:], TINY)
         ones = consts.tile([P, ONES_COLS], BF16, name="ones")
         nc.vector.memset(ones[:], 1.0)
         ident = consts.tile([P, P], F32, name="ident")
@@ -83,12 +90,6 @@ def tile_gcn_pa_kernel(tc, batch_graph, adj, W1, b1, out):
         w_grouped = consts.tile([P, F_OUT, PACK], BF16, name="w_grouped", align_bytes=64)
         w_codes = consts.tile([P, F_OUT], U32, name="w_codes", align_bytes=64)
         w_scales = consts.tile([P, F_OUT], U8, name="w_scales", align_bytes=64)
-        nc.vector.tensor_copy(out=w_grouped[:], in_=w_sb[:].rearrange("q t f -> q f t"))
-        nc.vector.quantize_mx(
-            out=w_codes[:].bitcast(FP8X4),
-            scales=w_scales[:],
-            in_=w_grouped[:].rearrange("q f t -> q (f t)"),
-        )
         bias = consts.tile([P, F_OUT], F32, name="bias")
 
         colsum = {}
@@ -109,30 +110,39 @@ def tile_gcn_pa_kernel(tc, batch_graph, adj, W1, b1, out):
         a_scales = {}
         out_acc = {}
 
-        def column_sums(g):
-            colsum[g] = psum.tile([P, PASSES, BLOCKS, ONES_COLS], F32, name="colsum", tag="acc", bufs=ACC_BANKS)
-            for c in range(PASSES):
-                for nb in range(BLOCKS):
-                    for t in range(PACK):
-                        nc.tensor.matmul(
-                            out=colsum[g][:, c, nb, :],
-                            lhsT=adj_sb[g][:, c * PACK + t, nb * P : (nb + 1) * P],
-                            rhs=ones[:],
-                            start=(t == 0),
-                            stop=(t == PACK - 1),
-                        )
+        def to_grouped_w():
+            nc.gpsimd.tensor_scalar(
+                out=w_grouped[:], in0=w_sb[:].rearrange("q t f -> q f t"), scalar1=1.0, scalar2=0.0, op0=ALU.mult, op1=ALU.add
+            )
 
-        def r_start(g):
+        def copy_out(engine, dst, bank):
+            if engine == "S":
+                nc.scalar.copy(out=dst, in_=bank)
+            else:
+                nc.vector.tensor_copy(out=dst, in_=bank)
+
+        def column_sums(g, c):
+            if c == 0:
+                colsum[g] = psum.tile([P, PASSES, BLOCKS, ONES_COLS], F32, name="colsum", tag="acc", bufs=ACC_BANKS)
+            for nb in range(BLOCKS):
+                for t in range(PACK):
+                    nc.tensor.matmul(
+                        out=colsum[g][:, c, nb, :],
+                        lhsT=adj_sb[g][:, c * PACK + t, nb * P : (nb + 1) * P],
+                        rhs=ones[:],
+                        start=(t == 0),
+                        stop=(t == PACK - 1),
+                    )
+
+        def r_sums(g):
             sums[g] = work.tile([P, BLOCKS], F32, name="sums")
-            is_zero = work.tile([P, BLOCKS], F32, name="is_zero")
-            safe = work.tile([P, BLOCKS], F32, name="safe")
-            root[g] = work.tile([P, BLOCKS], F32, name="root")
             nc.vector.tensor_reduce(
                 out=sums[g][:], in_=colsum[g][:, :, :, 0].rearrange("p c b -> p b c"), axis=AXIS.X, op=ALU.add
             )
-            nc.vector.tensor_single_scalar(out=is_zero[:], in_=sums[g][:], scalar=0.0, op=ALU.is_le)
-            nc.vector.tensor_tensor(out=safe[:], in0=sums[g][:], in1=is_zero[:], op=ALU.add)
-            nc.scalar.sqrt(out=root[g][:], in_=safe[:])
+
+        def r_root(g):
+            root[g] = work.tile([P, BLOCKS], F32, name="root")
+            nc.scalar.activation(out=root[g][:], in_=sums[g][:], func=ACT.Sqrt, bias=tiny[:])
 
         def r_finish(g):
             inv_root = work.tile([P, BLOCKS], F32, name="inv_root")
@@ -146,81 +156,81 @@ def tile_gcn_pa_kernel(tc, batch_graph, adj, W1, b1, out):
             r_row[g, hf] = psum.tile([P, BANK], F32, name="r_row", tag="r_row%d" % hf, bufs=1)
             for k in range(BANK // P):
                 b = hf * (BANK // P) + k
-                nc.tensor.matmul(
-                    out=r_row[g, hf][:, k * P : (k + 1) * P],
-                    lhsT=r_col[g][:, b : b + 1].to_broadcast([P, P]),
-                    rhs=ident[:],
+                nc.tensor.transpose(
+                    r_row[g, hf][:, k * P : (k + 1) * P], r_col[g][:, b : b + 1].to_broadcast([P, P]), ident[:]
+                )
+
+        def r_row_copy(g):
+            r_row_sb[g] = work.tile([P, BANK], F32, name="r_row_sb")
+            nc.scalar.copy(out=r_row_sb[g][:], in_=r_row[g, GPSIMD_HALF][:])
+
+        def x_transpose(g, pair, engine):
+            if pair == 0:
+                x_grouped[g] = work.tile([P, NODES * PACK], BF16, name="x_grouped", bufs=1, align_bytes=64)
+            x_words = x_grouped[g][:].bitcast(F32).rearrange("q (n u) -> q n u", u=2)
+            x_t = psum.tile([P, 2, 2, P], F32, name="x_t", tag="acc", bufs=ACC_BANKS)
+            for i in range(2):
+                words = x_sb[g][:, 2 * pair + i, :].bitcast(F32)
+                for u in range(2):
+                    nc.tensor.transpose(x_t[:, i, u, :], words[:, u * P : (u + 1) * P], ident[:])
+            copy_out(
+                engine,
+                x_words[:, pair * 2 * P : (pair + 1) * 2 * P, :].rearrange("q (i n) u -> q i n u", i=2),
+                x_t[:].rearrange("q i u n -> q i n u"),
+            )
+
+        def x_quantise(g, half):
+            if half == 0:
+                x_codes[g] = work.tile([P, NODES], U32, name="x_codes", align_bytes=64)
+                x_scales[g] = work.tile([P, NODES], U8, name="x_scales", align_bytes=64)
+            nodes = slice(half * BANK, (half + 1) * BANK)
+            nc.vector.quantize_mx(
+                out=x_codes[g][:, nodes].bitcast(FP8X4),
+                scales=x_scales[g][:, nodes],
+                in_=x_grouped[g][:, half * BANK * PACK : (half + 1) * BANK * PACK],
+            )
+
+        def h_matmul(g, c, fq, engine):
+            if (c, fq) == (0, 0):
+                h_grouped[g] = work.tile([P, PASSES, F_OUT, PACK], BF16, name="h_grouped", align_bytes=64)
+            f_cols = slice(fq * P, (fq + 1) * P)
+            h_acc = psum.tile([P, PACK, P], F32, name="h_acc", tag="acc", bufs=ACC_BANKS)
+            for t in range(PACK):
+                n_cols = slice((c * PACK + t) * P, (c * PACK + t + 1) * P)
+                nc.tensor.matmul_mx(
+                    out=h_acc[:, t, :],
+                    lhsT=x_codes[g][:, n_cols].bitcast(FP8X4),
+                    lhsT_scale=x_scales[g][:, n_cols],
+                    rhs=w_codes[:, f_cols].bitcast(FP8X4),
+                    rhs_scale=w_scales[:, f_cols],
                     start=True,
                     stop=True,
                 )
-            if hf == GPSIMD_HALF:
-                r_row_sb[g] = work.tile([P, BANK], F32, name="r_row_sb")
-                nc.scalar.copy(out=r_row_sb[g][:], in_=r_row[g, hf][:])
+            copy_out(engine, h_grouped[g][:, c, f_cols, :], h_acc[:].rearrange("p t f -> p f t"))
 
-        def x_transpose(g):
-            x_grouped[g] = work.tile([P, NODES * PACK], BF16, name="x_grouped", bufs=1, align_bytes=64)
-            x_words = x_grouped[g][:].bitcast(F32).rearrange("q (n u) -> q n u", u=2)
-            for pair in range(BLOCKS // 2):
-                x_t = psum.tile([P, 2, 2, P], F32, name="x_t", tag="acc", bufs=ACC_BANKS)
-                for i in range(2):
-                    words = x_sb[g][:, 2 * pair + i, :].bitcast(F32)
-                    for u in range(2):
-                        nc.tensor.transpose(x_t[:, i, u, :], words[:, u * P : (u + 1) * P], ident[:])
-                nc.scalar.copy(
-                    out=x_words[:, pair * 2 * P : (pair + 1) * 2 * P, :].rearrange("q (i n) u -> q i n u", i=2),
-                    in_=x_t[:].rearrange("q i u n -> q i n u"),
-                )
-
-        def x_quantise(g):
-            x_codes[g] = work.tile([P, NODES], U32, name="x_codes", align_bytes=64)
-            x_scales[g] = work.tile([P, NODES], U8, name="x_scales", align_bytes=64)
-            nc.vector.quantize_mx(out=x_codes[g][:].bitcast(FP8X4), scales=x_scales[g][:], in_=x_grouped[g][:])
-
-        def h_matmul(g, c):
+        def h_quantise(g, c):
             if c == 0:
-                h_grouped[g] = work.tile([P, PASSES, F_OUT, PACK], BF16, name="h_grouped", align_bytes=64)
-            for fq in range(F_OUT // P):
-                f_cols = slice(fq * P, (fq + 1) * P)
-                h_acc = psum.tile([P, PACK, P], F32, name="h_acc", tag="acc", bufs=ACC_BANKS)
-                for t in range(PACK):
-                    n_cols = slice((c * PACK + t) * P, (c * PACK + t + 1) * P)
-                    nc.tensor.matmul_mx(
-                        out=h_acc[:, t, :],
-                        lhsT=x_codes[g][:, n_cols].bitcast(FP8X4),
-                        lhsT_scale=x_scales[g][:, n_cols],
-                        rhs=w_codes[:, f_cols].bitcast(FP8X4),
-                        rhs_scale=w_scales[:, f_cols],
-                        start=True,
-                        stop=True,
-                    )
-                nc.scalar.copy(out=h_grouped[g][:, c, f_cols, :], in_=h_acc[:].rearrange("p t f -> p f t"))
-
-        def h_quantise(g):
-            h_codes[g] = work.tile([P, PASSES, F_OUT], U32, name="h_codes", align_bytes=64)
-            h_scales[g] = work.tile([P, PASSES, F_OUT], U8, name="h_scales", align_bytes=64)
+                h_codes[g] = work.tile([P, PASSES, F_OUT], U32, name="h_codes", align_bytes=64)
+                h_scales[g] = work.tile([P, PASSES, F_OUT], U8, name="h_scales", align_bytes=64)
             nc.vector.quantize_mx(
-                out=h_codes[g][:].rearrange("p c f -> p (c f)").bitcast(FP8X4),
-                scales=h_scales[g][:].rearrange("p c f -> p (c f)"),
-                in_=h_grouped[g][:].rearrange("p c f t -> p (c f t)"),
+                out=h_codes[g][:, c, :].bitcast(FP8X4),
+                scales=h_scales[g][:, c, :],
+                in_=h_grouped[g][:, c, :, :].rearrange("p f t -> p (f t)"),
             )
 
-        def scale_planes(g, c):
-            planes[g, c] = work.tile([P, PACK, NODES], F32, name="planes", bufs=3)
-            for t in range(PACK):
-                b = c * PACK + t
-                if t < SCALAR_PLANES:
-                    nc.scalar.activation(
-                        out=planes[g, c][:, t, :], in_=adj_sb[g][:, b, :], func=ACT.Copy, scale=r_col[g][:, b : b + 1]
-                    )
-                else:
-                    nc.gpsimd.tensor_scalar(
-                        out=planes[g, c][:, t, :],
-                        in0=adj_sb[g][:, b, :],
-                        scalar1=r_col[g][:, b : b + 1],
-                        scalar2=0.0,
-                        op0=ALU.mult,
-                        op1=ALU.add,
-                    )
+        def scale_plane(g, c, t, engine):
+            if (g, c) not in planes:
+                planes[g, c] = work.tile([P, PACK, NODES], F32, name="planes", bufs=3)
+            b = c * PACK + t
+            dst = planes[g, c][:, t, :]
+            src = adj_sb[g][:, b, :]
+            r_j = r_col[g][:, b : b + 1]
+            if engine == "S":
+                nc.scalar.activation(out=dst, in_=src, func=ACT.Copy, scale=r_j)
+            elif engine == "V":
+                nc.vector.tensor_scalar(out=dst, in0=src, scalar1=r_j, scalar2=None, op0=ALU.mult)
+            else:
+                nc.gpsimd.tensor_scalar(out=dst, in0=src, scalar1=r_j, scalar2=0.0, op0=ALU.mult, op1=ALU.add)
 
         def a_multiply(g, c, hf):
             a_grouped[g, c, hf] = work.tile([P, BANK, PACK], BF16, name="a_grouped", bufs=2, align_bytes=64)
@@ -234,18 +244,21 @@ def tile_gcn_pa_kernel(tc, batch_graph, adj, W1, b1, out):
                 op=ALU.mult,
             )
 
-        def a_multiply_gpsimd(g):
+        def a_multiply_gpsimd(g, part):
             c, hf = PASSES - 1, GPSIMD_HALF
-            a_grouped[g, c, hf] = work.tile([P, BANK, PACK], BF16, name="a_grouped_gp", bufs=1, align_bytes=64)
+            if part == 0:
+                a_grouped[g, c, hf] = work.tile([P, BANK, PACK], BF16, name="a_grouped_gp", bufs=1, align_bytes=64)
+            w = BANK // GP_PARTS
+            cols = slice(part * w, (part + 1) * w)
             nc.gpsimd.tensor_tensor(
-                out=a_grouped[g, c, hf][:],
-                in0=planes[g, c][:, :, hf * BANK : (hf + 1) * BANK].rearrange("p t i -> p i t"),
-                in1=r_row_sb[g][:].unsqueeze(2).to_broadcast([P, BANK, PACK]),
+                out=a_grouped[g, c, hf][:, cols, :],
+                in0=planes[g, c][:, :, hf * BANK + part * w : hf * BANK + (part + 1) * w].rearrange("p t i -> p i t"),
+                in1=r_row_sb[g][:, cols].unsqueeze(2).to_broadcast([P, w, PACK]),
                 op=ALU.mult,
             )
 
         def a_quantise(g, c, hf):
-            if (c, hf) == (0, 0):
+            if g not in a_codes:
                 a_codes[g] = work.tile([P, PASSES, NODES], U32, name="a_codes", align_bytes=64)
                 a_scales[g] = work.tile([P, PASSES, NODES], U8, name="a_scales", align_bytes=64)
             cols = slice(hf * BANK, (hf + 1) * BANK)
@@ -255,81 +268,133 @@ def tile_gcn_pa_kernel(tc, batch_graph, adj, W1, b1, out):
                 in_=a_grouped[g, c, hf][:].rearrange("p i t -> p (i t)"),
             )
 
-        def out_matmul(g, st):
-            for k in range(STORE_BLOCKS):
-                i_cols = slice((st * STORE_BLOCKS + k) * P, (st * STORE_BLOCKS + k + 1) * P)
-                out_acc[g, st, k] = psum.tile([P, F_OUT], F32, name="out_acc", tag="acc", bufs=ACC_BANKS)
-                for c in range(PASSES):
-                    nc.tensor.matmul_mx(
-                        out=out_acc[g, st, k][:],
-                        lhsT=a_codes[g][:, c, i_cols].bitcast(FP8X4),
-                        lhsT_scale=a_scales[g][:, c, i_cols],
-                        rhs=h_codes[g][:, c, :].bitcast(FP8X4),
-                        rhs_scale=h_scales[g][:, c, :],
-                        start=(c == 0),
-                        stop=(c == PASSES - 1),
-                    )
+        def out_matmul(g, block):
+            i_cols = slice(block * P, (block + 1) * P)
+            out_acc[g, block] = psum.tile([P, F_OUT], F32, name="out_acc", tag="acc", bufs=ACC_BANKS)
+            for c in range(PASSES):
+                nc.tensor.matmul_mx(
+                    out=out_acc[g, block][:],
+                    lhsT=a_codes[g][:, c, i_cols].bitcast(FP8X4),
+                    lhsT_scale=a_scales[g][:, c, i_cols],
+                    rhs=h_codes[g][:, c, :].bitcast(FP8X4),
+                    rhs_scale=h_scales[g][:, c, :],
+                    start=(c == 0),
+                    stop=(c == PASSES - 1),
+                )
 
-        def out_finish(g, st):
-            result = work.tile([P, STORE_BLOCKS, F_OUT], F32, name="result", bufs=4)
-            for k in range(STORE_BLOCKS):
-                block = st * STORE_BLOCKS + k
-                nc.vector.tensor_tensor(out=result[:, k, :], in0=out_acc[g, st, k][:], in1=bias[:], op=ALU.add)
-                nc.scalar.activation(out=result[:, k, :], in_=result[:, k, :], func=ACT.Relu)
-                nc.sync.dma_start(out=out[g, block * P : (block + 1) * P, :], in_=result[:, k, :])
+        def out_finish(g, block):
+            result = work.tile([P, F_OUT], F32, name="result", bufs=8)
+            nc.vector.tensor_tensor(out=result[:], in0=out_acc[g, block][:], in1=bias[:], op=ALU.add)
+            nc.scalar.activation(out=result[:], in_=result[:], func=ACT.Relu)
+            nc.sync.dma_start(out=out[g, block * P : (block + 1) * P, :], in_=result[:])
 
-        column_sums(0)
-        r_start(0)
-        x_transpose(0)
+        nc.vector.tensor_copy(out=w_grouped[:], in_=w_sb[:].rearrange("q t f -> q f t"))
+        x_transpose(0, 0, "S")
+        x_transpose(0, 1, "S")
+        nc.vector.quantize_mx(
+            out=w_codes[:].bitcast(FP8X4),
+            scales=w_scales[:],
+            in_=w_grouped[:].rearrange("q f t -> q (f t)"),
+        )
+        x_transpose(0, 2, "S")
+        x_transpose(0, 3, "V")
+        load_x(2)
+        load_adj(2)
+        x_quantise(0, 0)
+        for fq in range(FQ):
+            h_matmul(0, 0, fq, "SVSV"[fq])
+            if fq == 1:
+                x_quantise(0, 1)
+        column_sums(0, 0)
+        column_sums(0, 1)
+        for fq in range(2):
+            h_matmul(0, 1, fq, "SV"[fq])
+        r_sums(0)
+        r_root(0)
+        for fq in range(2, 4):
+            h_matmul(0, 1, fq, "VV"[fq - 2])
         r_finish(0)
-        scale_planes(0, 0)
+        for t in range(PACK):
+            scale_plane(0, 0, t, "SVVS"[t])
         r_rows(0, 0)
+        h_quantise(0, 0)
+        h_quantise(0, 1)
+        for t in range(PACK):
+            scale_plane(0, 1, t, "SSGG"[t])
         r_rows(0, 1)
-        scale_planes(0, 1)
-        a_multiply_gpsimd(0)
+        for pair in range(PAIRS):
+            x_transpose(1, pair, "S")
         load_x(3)
         load_adj(3)
-        x_quantise(0)
         nc.vector.tensor_copy(out=bias[:], in_=bias_bf[:])
-        x_transpose(1)
-        column_sums(1)
-        h_matmul(0, 0)
-        h_matmul(0, 1)
+        r_row_copy(0)
+        column_sums(1, 0)
+        column_sums(1, 1)
 
         for g in range(GRAPHS):
             nxt = g + 1
             more = nxt < GRAPHS
             more2 = nxt + 1 < GRAPHS
             a_multiply(g, 0, 0)
+            if g == 0:
+                r_sums(1)
+                r_root(1)
+            for part in range(GP_PARTS):
+                a_multiply_gpsimd(g, part)
+            if g > 0:
+                if more:
+                    for t in range(PACK):
+                        scale_plane(nxt, 0, t, "SSGG"[t])
+                for block in range(4, 8):
+                    out_finish(g - 1, block)
+                h_quantise(g, 0)
+                h_quantise(g, 1)
+            else:
+                r_finish(1)
+                for t in range(PACK):
+                    scale_plane(1, 0, t, "SSGG"[t])
             if more:
-                x_quantise(nxt)
-                r_start(nxt)
-                h_matmul(nxt, 0)
-                h_matmul(nxt, 1)
+                x_quantise(nxt, 0)
+                x_quantise(nxt, 1)
+                for fq in range(FQ):
+                    h_matmul(nxt, 0, fq, "S")
+            a_multiply(g, 1, 0)
+            if more:
+                r_rows(nxt, 0)
+            if more2:
+                column_sums(nxt + 1, 0)
+                column_sums(nxt + 1, 1)
+            a_quantise(g, 0, 0)
+            if more2:
+                r_sums(nxt + 1)
+                r_root(nxt + 1)
+            a_quantise(g, 1, 0)
+            for block in range(4):
+                out_matmul(g, block)
             a_multiply(g, 0, 1)
             if more:
-                r_finish(nxt)
-                scale_planes(nxt, 0)
-                r_rows(nxt, 0)
-                scale_planes(nxt, 1)
-            a_quantise(g, 0, 0)
-            a_quantise(g, 1, 0)
-            h_quantise(g)
-            out_matmul(g, 0)
-            out_matmul(g, 1)
-            a_multiply(g, 1, 1)
-            a_quantise(g, 0, 1)
-            a_quantise(g, 1, 1)
-            out_matmul(g, 2)
+                for t in range(PACK):
+                    scale_plane(nxt, 1, t, "SSGG"[t])
+                r_rows(nxt, 1)
+                for fq in range(FQ):
+                    h_matmul(nxt, 1, fq, "S")
             out_finish(g, 0)
-            out_matmul(g, 3)
-            if more2:
-                x_transpose(nxt + 1)
             out_finish(g, 1)
             if more:
-                a_multiply_gpsimd(nxt)
-                r_rows(nxt, 1)
+                r_row_copy(nxt)
+                out_finish(g, 2)
+                out_finish(g, 3)
+            a_quantise(g, 0, 1)
+            a_quantise(g, 1, 1)
             if more2:
-                column_sums(nxt + 1)
-            out_finish(g, 2)
-            out_finish(g, 3)
+                r_finish(nxt + 1)
+            if more2:
+                for pair in range(PAIRS):
+                    x_transpose(nxt + 1, pair, "S")
+            for block in range(4, 8):
+                out_matmul(g, block)
+            if not more:
+                out_finish(g, 2)
+                out_finish(g, 3)
+                for block in range(4, 8):
+                    out_finish(g, block)

@@ -25,10 +25,14 @@ HALVES = NODES // BANK
 ONES_COLS = 32
 TINY = 2.0**-126
 RUN = 4
-GP_PARTS = 4
+GP_COLS = 64
+LAST_COLS = 256
 GPSIMD_HALF = 1
 PAIRS = BLOCKS // 2
 FQ = F_OUT // P
+X_BUFS = 2
+PLANES_BUFS = 4
+RESULT_BUFS = 8
 INPUT_BUFS = 3
 ACC_BANKS = 6
 
@@ -38,7 +42,7 @@ FLOPS = 2 * GRAPHS * NODES * F_IN * F_OUT + 2 * GRAPHS * NODES * NODES * F_OUT
 def tile_gcn_pa_kernel(tc, batch_graph, adj, W1, b1, out):
     nc = tc.nc
     with ExitStack() as ctx:
-        ctx.enter_context(tc.manual_schedule(engines={mybir.EngineType.SP}))
+        ctx.enter_context(tc.manual_schedule())
         consts = ctx.enter_context(tc.tile_pool(name="consts", bufs=1))
         inputs = ctx.enter_context(tc.tile_pool(name="inputs", bufs=INPUT_BUFS))
         work = ctx.enter_context(tc.tile_pool(name="work", bufs=2))
@@ -59,7 +63,7 @@ def tile_gcn_pa_kernel(tc, batch_graph, adj, W1, b1, out):
                 )
 
         def load_x(g):
-            x_sb[g] = inputs.tile([P, BLOCKS, F_IN], BF16, name="x_sb", tag="x_sb", bufs=2)
+            x_sb[g] = inputs.tile([P, BLOCKS, F_IN], BF16, name="x_sb", tag="x_sb", bufs=X_BUFS)
             half = BLOCKS // 2
             for k in range(2):
                 rows = batch_graph[g, k * half * P : (k + 1) * half * P, :]
@@ -95,10 +99,13 @@ def tile_gcn_pa_kernel(tc, batch_graph, adj, W1, b1, out):
         colsum = {}
         sums = {}
         root = {}
+        inv_root = {}
         r_col = {}
         r_row = {}
         r_row_sb = {}
         x_grouped = {}
+        x_turned = {}
+        h_acc = {}
         x_codes = {}
         x_scales = {}
         h_grouped = {}
@@ -109,11 +116,7 @@ def tile_gcn_pa_kernel(tc, batch_graph, adj, W1, b1, out):
         a_codes = {}
         a_scales = {}
         out_acc = {}
-
-        def to_grouped_w():
-            nc.gpsimd.tensor_scalar(
-                out=w_grouped[:], in0=w_sb[:].rearrange("q t f -> q f t"), scalar1=1.0, scalar2=0.0, op0=ALU.mult, op1=ALU.add
-            )
+        result = {}
 
         def copy_out(engine, dst, bank):
             if engine == "S":
@@ -144,12 +147,14 @@ def tile_gcn_pa_kernel(tc, batch_graph, adj, W1, b1, out):
             root[g] = work.tile([P, BLOCKS], F32, name="root")
             nc.scalar.activation(out=root[g][:], in_=sums[g][:], func=ACT.Sqrt, bias=tiny[:])
 
+        def r_invert(g):
+            inv_root[g] = work.tile([P, BLOCKS], F32, name="inv_root")
+            nc.vector.reciprocal(out=inv_root[g][:], in_=root[g][:])
+
         def r_finish(g):
-            inv_root = work.tile([P, BLOCKS], F32, name="inv_root")
             r_col[g] = work.tile([P, BLOCKS], F32, name="r_col")
-            nc.vector.reciprocal(out=inv_root[:], in_=root[g][:])
             nc.vector.scalar_tensor_tensor(
-                out=r_col[g][:], in0=sums[g][:], scalar=0.0, in1=inv_root[:], op0=ALU.is_gt, op1=ALU.mult
+                out=r_col[g][:], in0=sums[g][:], scalar=0.0, in1=inv_root[g][:], op0=ALU.is_gt, op1=ALU.mult
             )
 
         def r_rows(g, hf):
@@ -164,41 +169,44 @@ def tile_gcn_pa_kernel(tc, batch_graph, adj, W1, b1, out):
             r_row_sb[g] = work.tile([P, BANK], F32, name="r_row_sb")
             nc.scalar.copy(out=r_row_sb[g][:], in_=r_row[g, GPSIMD_HALF][:])
 
-        def x_transpose(g, pair, engine):
+        def x_transpose(g, pair):
             if pair == 0:
                 x_grouped[g] = work.tile([P, NODES * PACK], BF16, name="x_grouped", bufs=1, align_bytes=64)
-            x_words = x_grouped[g][:].bitcast(F32).rearrange("q (n u) -> q n u", u=2)
             x_t = psum.tile([P, 2, 2, P], F32, name="x_t", tag="acc", bufs=ACC_BANKS)
             for i in range(2):
                 words = x_sb[g][:, 2 * pair + i, :].bitcast(F32)
                 for u in range(2):
                     nc.tensor.transpose(x_t[:, i, u, :], words[:, u * P : (u + 1) * P], ident[:])
+            x_turned[g, pair] = x_t
+
+        def x_copy(g, pair, engine):
+            x_words = x_grouped[g][:].bitcast(F32).rearrange("q (n u) -> q n u", u=2)
             copy_out(
                 engine,
                 x_words[:, pair * 2 * P : (pair + 1) * 2 * P, :].rearrange("q (i n) u -> q i n u", i=2),
-                x_t[:].rearrange("q i u n -> q i n u"),
+                x_turned[g, pair][:].rearrange("q i u n -> q i n u"),
             )
 
-        def x_quantise(g, half):
-            if half == 0:
-                x_codes[g] = work.tile([P, NODES], U32, name="x_codes", align_bytes=64)
-                x_scales[g] = work.tile([P, NODES], U8, name="x_scales", align_bytes=64)
-            nodes = slice(half * BANK, (half + 1) * BANK)
+        def x_quantise(g, lo=0, hi=NODES):
+            if lo == 0:
+                x_codes[g] = work.tile([P, NODES], U32, name="x_codes", bufs=1, align_bytes=64)
+                x_scales[g] = work.tile([P, NODES], U8, name="x_scales", bufs=1, align_bytes=64)
+            nodes = slice(lo, hi)
             nc.vector.quantize_mx(
                 out=x_codes[g][:, nodes].bitcast(FP8X4),
                 scales=x_scales[g][:, nodes],
-                in_=x_grouped[g][:, half * BANK * PACK : (half + 1) * BANK * PACK],
+                in_=x_grouped[g][:, lo * PACK : hi * PACK],
             )
 
-        def h_matmul(g, c, fq, engine):
+        def h_matmul(g, c, fq):
             if (c, fq) == (0, 0):
-                h_grouped[g] = work.tile([P, PASSES, F_OUT, PACK], BF16, name="h_grouped", align_bytes=64)
+                h_grouped[g] = work.tile([P, PASSES, F_OUT, PACK], BF16, name="h_grouped", bufs=1, align_bytes=64)
             f_cols = slice(fq * P, (fq + 1) * P)
-            h_acc = psum.tile([P, PACK, P], F32, name="h_acc", tag="acc", bufs=ACC_BANKS)
+            h_acc[g, c, fq] = psum.tile([P, PACK, P], F32, name="h_acc", tag="acc", bufs=ACC_BANKS)
             for t in range(PACK):
                 n_cols = slice((c * PACK + t) * P, (c * PACK + t + 1) * P)
                 nc.tensor.matmul_mx(
-                    out=h_acc[:, t, :],
+                    out=h_acc[g, c, fq][:, t, :],
                     lhsT=x_codes[g][:, n_cols].bitcast(FP8X4),
                     lhsT_scale=x_scales[g][:, n_cols],
                     rhs=w_codes[:, f_cols].bitcast(FP8X4),
@@ -206,21 +214,27 @@ def tile_gcn_pa_kernel(tc, batch_graph, adj, W1, b1, out):
                     start=True,
                     stop=True,
                 )
-            copy_out(engine, h_grouped[g][:, c, f_cols, :], h_acc[:].rearrange("p t f -> p f t"))
 
-        def h_quantise(g, c):
-            if c == 0:
+        def h_copy(g, c, fq, engine):
+            copy_out(
+                engine,
+                h_grouped[g][:, c, fq * P : (fq + 1) * P, :],
+                h_acc[g, c, fq][:].rearrange("p t f -> p f t"),
+            )
+
+        def h_quantise(g):
+            if True:
                 h_codes[g] = work.tile([P, PASSES, F_OUT], U32, name="h_codes", align_bytes=64)
                 h_scales[g] = work.tile([P, PASSES, F_OUT], U8, name="h_scales", align_bytes=64)
             nc.vector.quantize_mx(
-                out=h_codes[g][:, c, :].bitcast(FP8X4),
-                scales=h_scales[g][:, c, :],
-                in_=h_grouped[g][:, c, :, :].rearrange("p f t -> p (f t)"),
+                out=h_codes[g][:].rearrange("p c f -> p (c f)").bitcast(FP8X4),
+                scales=h_scales[g][:].rearrange("p c f -> p (c f)"),
+                in_=h_grouped[g][:].rearrange("p c f t -> p (c f t)"),
             )
 
         def scale_plane(g, c, t, engine):
             if (g, c) not in planes:
-                planes[g, c] = work.tile([P, PACK, NODES], F32, name="planes", bufs=3)
+                planes[g, c] = work.tile([P, PACK, NODES], F32, name="planes", bufs=PLANES_BUFS)
             b = c * PACK + t
             dst = planes[g, c][:, t, :]
             src = adj_sb[g][:, b, :]
@@ -230,103 +244,123 @@ def tile_gcn_pa_kernel(tc, batch_graph, adj, W1, b1, out):
             elif engine == "V":
                 nc.vector.tensor_scalar(out=dst, in0=src, scalar1=r_j, scalar2=None, op0=ALU.mult)
             else:
-                nc.gpsimd.tensor_scalar(out=dst, in0=src, scalar1=r_j, scalar2=0.0, op0=ALU.mult, op1=ALU.add)
+                for half in (slice(0, BANK), slice(BANK, NODES)):
+                    nc.gpsimd.tensor_scalar(
+                        out=dst[:, half], in0=src[:, half], scalar1=r_j, scalar2=0.0, op0=ALU.mult, op1=ALU.add
+                    )
+
+        def gp_cols(g, c, hf):
+            if (c, hf) == (PASSES - 1, GPSIMD_HALF):
+                return BANK
+            if (g, c, hf) == (GRAPHS - 1, 0, GPSIMD_HALF):
+                return LAST_COLS
+            return 0
+
+        def a_tile(g, hf):
+            if (g, hf) not in a_grouped:
+                a_grouped[g, hf] = work.tile([P, PASSES, BANK, PACK], BF16, name="a_grouped", bufs=2, align_bytes=64)
 
         def a_multiply(g, c, hf):
-            a_grouped[g, c, hf] = work.tile([P, BANK, PACK], BF16, name="a_grouped", bufs=2, align_bytes=64)
+            a_tile(g, hf)
+            w = BANK - gp_cols(g, c, hf)
             nc.vector.tensor_tensor(
-                out=a_grouped[g, c, hf][:].rearrange("p (n i) t -> p n t i", i=RUN),
-                in0=planes[g, c][:, :, hf * BANK : (hf + 1) * BANK].rearrange("p t (n i) -> p n t i", i=RUN),
-                in1=r_row[g, hf][:]
+                out=a_grouped[g, hf][:, c, :w, :].rearrange("p (n i) t -> p n t i", i=RUN),
+                in0=planes[g, c][:, :, hf * BANK : hf * BANK + w].rearrange("p t (n i) -> p n t i", i=RUN),
+                in1=r_row[g, hf][:, :w]
                 .rearrange("p (n i) -> p n i", i=RUN)
                 .unsqueeze(2)
-                .to_broadcast([P, BANK // RUN, PACK, RUN]),
+                .to_broadcast([P, w // RUN, PACK, RUN]),
                 op=ALU.mult,
             )
 
-        def a_multiply_gpsimd(g, part):
-            c, hf = PASSES - 1, GPSIMD_HALF
-            if part == 0:
-                a_grouped[g, c, hf] = work.tile([P, BANK, PACK], BF16, name="a_grouped_gp", bufs=1, align_bytes=64)
-            w = BANK // GP_PARTS
-            cols = slice(part * w, (part + 1) * w)
-            nc.gpsimd.tensor_tensor(
-                out=a_grouped[g, c, hf][:, cols, :],
-                in0=planes[g, c][:, :, hf * BANK + part * w : hf * BANK + (part + 1) * w].rearrange("p t i -> p i t"),
-                in1=r_row_sb[g][:, cols].unsqueeze(2).to_broadcast([P, w, PACK]),
-                op=ALU.mult,
-            )
+        def a_multiply_gpsimd(g, c):
+            hf = GPSIMD_HALF
+            a_tile(g, hf)
+            for lo in range(BANK - gp_cols(g, c, hf), BANK, GP_COLS):
+                nc.gpsimd.tensor_tensor(
+                    out=a_grouped[g, hf][:, c, lo : lo + GP_COLS, :],
+                    in0=planes[g, c][:, :, hf * BANK + lo : hf * BANK + lo + GP_COLS].rearrange("p t i -> p i t"),
+                    in1=r_row_sb[g][:, lo : lo + GP_COLS].unsqueeze(2).to_broadcast([P, GP_COLS, PACK]),
+                    op=ALU.mult,
+                )
 
-        def a_quantise(g, c, hf):
-            if g not in a_codes:
-                a_codes[g] = work.tile([P, PASSES, NODES], U32, name="a_codes", align_bytes=64)
-                a_scales[g] = work.tile([P, PASSES, NODES], U8, name="a_scales", align_bytes=64)
-            cols = slice(hf * BANK, (hf + 1) * BANK)
+        def a_quantise(g, hf):
+            a_codes[g, hf] = work.tile([P, PASSES, BANK], U32, name="a_codes", bufs=4, align_bytes=64)
+            a_scales[g, hf] = work.tile([P, PASSES, BANK], U8, name="a_scales", bufs=4, align_bytes=64)
             nc.vector.quantize_mx(
-                out=a_codes[g][:, c, cols].bitcast(FP8X4),
-                scales=a_scales[g][:, c, cols],
-                in_=a_grouped[g, c, hf][:].rearrange("p i t -> p (i t)"),
+                out=a_codes[g, hf][:].rearrange("p c i -> p (c i)").bitcast(FP8X4),
+                scales=a_scales[g, hf][:].rearrange("p c i -> p (c i)"),
+                in_=a_grouped[g, hf][:].rearrange("p c i t -> p (c i t)"),
             )
 
         def out_matmul(g, block):
-            i_cols = slice(block * P, (block + 1) * P)
+            hf, k = divmod(block, BANK // P)
+            i_cols = slice(k * P, (k + 1) * P)
             out_acc[g, block] = psum.tile([P, F_OUT], F32, name="out_acc", tag="acc", bufs=ACC_BANKS)
             for c in range(PASSES):
                 nc.tensor.matmul_mx(
                     out=out_acc[g, block][:],
-                    lhsT=a_codes[g][:, c, i_cols].bitcast(FP8X4),
-                    lhsT_scale=a_scales[g][:, c, i_cols],
+                    lhsT=a_codes[g, hf][:, c, i_cols].bitcast(FP8X4),
+                    lhsT_scale=a_scales[g, hf][:, c, i_cols],
                     rhs=h_codes[g][:, c, :].bitcast(FP8X4),
                     rhs_scale=h_scales[g][:, c, :],
                     start=(c == 0),
                     stop=(c == PASSES - 1),
                 )
 
-        def out_finish(g, block):
-            result = work.tile([P, F_OUT], F32, name="result", bufs=8)
-            nc.vector.tensor_tensor(out=result[:], in0=out_acc[g, block][:], in1=bias[:], op=ALU.add)
-            nc.scalar.activation(out=result[:], in_=result[:], func=ACT.Relu)
-            nc.sync.dma_start(out=out[g, block * P : (block + 1) * P, :], in_=result[:])
+        def out_add(g, block):
+            result[g, block] = work.tile([P, F_OUT], F32, name="result", bufs=RESULT_BUFS)
+            nc.vector.tensor_tensor(out=result[g, block][:], in0=out_acc[g, block][:], in1=bias[:], op=ALU.add)
+
+        def out_relu(g, block):
+            res = result[g, block][:]
+            nc.scalar.activation(out=res, in_=res, func=ACT.Relu)
+            nc.sync.dma_start(out=out[g, block * P : (block + 1) * P, :], in_=res)
 
         nc.vector.tensor_copy(out=w_grouped[:], in_=w_sb[:].rearrange("q t f -> q f t"))
-        x_transpose(0, 0, "S")
-        x_transpose(0, 1, "S")
+        for pair in range(PAIRS):
+            x_transpose(0, pair)
+        for pair in range(3):
+            x_copy(0, pair, "S")
         nc.vector.quantize_mx(
             out=w_codes[:].bitcast(FP8X4),
             scales=w_scales[:],
             in_=w_grouped[:].rearrange("q f t -> q (f t)"),
         )
-        x_transpose(0, 2, "S")
-        x_transpose(0, 3, "V")
+        x_quantise(0, 0, BANK)
+        x_copy(0, 3, "V")
         load_x(2)
         load_adj(2)
-        x_quantise(0, 0)
         for fq in range(FQ):
-            h_matmul(0, 0, fq, "SVSV"[fq])
-            if fq == 1:
-                x_quantise(0, 1)
+            h_matmul(0, 0, fq)
+        x_quantise(0, BANK, NODES)
+        for fq in range(FQ):
+            h_copy(0, 0, fq, "SV"[fq % 2])
         column_sums(0, 0)
         column_sums(0, 1)
-        for fq in range(2):
-            h_matmul(0, 1, fq, "SV"[fq])
+        for fq in range(FQ):
+            h_matmul(0, 1, fq)
         r_sums(0)
         r_root(0)
-        for fq in range(2, 4):
-            h_matmul(0, 1, fq, "VV"[fq - 2])
-        r_finish(0)
-        for t in range(PACK):
-            scale_plane(0, 0, t, "SVVS"[t])
-        r_rows(0, 0)
-        h_quantise(0, 0)
-        h_quantise(0, 1)
-        for t in range(PACK):
-            scale_plane(0, 1, t, "SSGG"[t])
-        r_rows(0, 1)
-        for pair in range(PAIRS):
-            x_transpose(1, pair, "S")
-        load_x(3)
-        load_adj(3)
         nc.vector.tensor_copy(out=bias[:], in_=bias_bf[:])
+        h_copy(0, 1, 0, "S")
+        r_invert(0)
+        h_copy(0, 1, 1, "V")
+        r_finish(0)
+        scale_plane(0, 0, 0, "S")
+        scale_plane(0, 0, 1, "V")
+        scale_plane(0, 0, 2, "V")
+        scale_plane(0, 0, 3, "V")
+        r_rows(0, 0)
+        r_rows(0, 1)
+        h_copy(0, 1, 2, "S")
+        h_copy(0, 1, 3, "S")
+        scale_plane(0, 1, 2, "G")
+        scale_plane(0, 1, 3, "G")
+        for pair in range(PAIRS):
+            x_transpose(1, pair)
+        scale_plane(0, 1, 0, "S")
+        scale_plane(0, 1, 1, "S")
         r_row_copy(0)
         column_sums(1, 0)
         column_sums(1, 1)
@@ -337,64 +371,74 @@ def tile_gcn_pa_kernel(tc, batch_graph, adj, W1, b1, out):
             more2 = nxt + 1 < GRAPHS
             a_multiply(g, 0, 0)
             if g == 0:
+                load_x(3)
+                load_adj(3)
+            if g > 0:
+                for fq in range(FQ):
+                    h_copy(g, 1, fq, "S")
+                for block in range(4, 8):
+                    out_add(g - 1, block)
+                    out_relu(g - 1, block)
+                h_quantise(g)
+            if g == 0:
+                h_quantise(0)
+            a_multiply_gpsimd(g, 0)
+            a_multiply_gpsimd(g, 1)
+            if more:
+                if g > 0:
+                    for pair in range(PAIRS):
+                        x_transpose(nxt, pair)
+                for pair in range(PAIRS):
+                    x_copy(nxt, pair, "S")
+            if g == 0:
                 r_sums(1)
                 r_root(1)
-            for part in range(GP_PARTS):
-                a_multiply_gpsimd(g, part)
-            if g > 0:
-                if more:
-                    for t in range(PACK):
-                        scale_plane(nxt, 0, t, "SSGG"[t])
-                for block in range(4, 8):
-                    out_finish(g - 1, block)
-                h_quantise(g, 0)
-                h_quantise(g, 1)
-            else:
-                r_finish(1)
-                for t in range(PACK):
-                    scale_plane(1, 0, t, "SSGG"[t])
-            if more:
-                x_quantise(nxt, 0)
-                x_quantise(nxt, 1)
-                for fq in range(FQ):
-                    h_matmul(nxt, 0, fq, "S")
-            a_multiply(g, 1, 0)
-            if more:
-                r_rows(nxt, 0)
             if more2:
                 column_sums(nxt + 1, 0)
                 column_sums(nxt + 1, 1)
-            a_quantise(g, 0, 0)
+            a_multiply(g, 1, 0)
+            if g == 0:
+                r_invert(1)
+            if more:
+                x_quantise(nxt)
+            if g == 0:
+                r_finish(1)
+            if more:
+                scale_plane(nxt, 0, 0, "S")
+                scale_plane(nxt, 0, 1, "S")
+                scale_plane(nxt, 0, 2, "G")
+                scale_plane(nxt, 0, 3, "G")
+                r_rows(nxt, 0)
+                for fq in range(FQ):
+                    h_matmul(nxt, 0, fq)
+                    h_copy(nxt, 0, fq, "S")
             if more2:
                 r_sums(nxt + 1)
                 r_root(nxt + 1)
-            a_quantise(g, 1, 0)
+            a_quantise(g, 0)
             for block in range(4):
                 out_matmul(g, block)
             a_multiply(g, 0, 1)
             if more:
-                for t in range(PACK):
-                    scale_plane(nxt, 1, t, "SSGG"[t])
+                scale_plane(nxt, 1, 0, "S")
+                scale_plane(nxt, 1, 1, "S")
+                scale_plane(nxt, 1, 2, "G")
+                scale_plane(nxt, 1, 3, "G")
                 r_rows(nxt, 1)
-                for fq in range(FQ):
-                    h_matmul(nxt, 1, fq, "S")
-            out_finish(g, 0)
-            out_finish(g, 1)
+            for block in range(4 if more else 2):
+                out_add(g, block)
+                out_relu(g, block)
+            if more2:
+                r_invert(nxt + 1)
             if more:
                 r_row_copy(nxt)
-                out_finish(g, 2)
-                out_finish(g, 3)
-            a_quantise(g, 0, 1)
-            a_quantise(g, 1, 1)
+                for fq in range(FQ):
+                    h_matmul(nxt, 1, fq)
+            a_quantise(g, 1)
             if more2:
                 r_finish(nxt + 1)
-            if more2:
-                for pair in range(PAIRS):
-                    x_transpose(nxt + 1, pair, "S")
             for block in range(4, 8):
                 out_matmul(g, block)
-            if not more:
-                out_finish(g, 2)
-                out_finish(g, 3)
-                for block in range(4, 8):
-                    out_finish(g, block)
+        for block in range(2, 8):
+            out_add(GRAPHS - 1, block)
+            out_relu(GRAPHS - 1, block)

@@ -25,8 +25,6 @@ HALVES = NODES // BANK
 ONES_COLS = 32
 TINY = 2.0**-126
 RUN = 4
-GP_COLS = 64
-LAST_COLS = 256
 GPSIMD_HALF = 1
 PAIRS = BLOCKS // 2
 FQ = F_OUT // P
@@ -151,18 +149,23 @@ def tile_gcn_pa_kernel(tc, batch_graph, adj, W1, b1, out):
             inv_root[g] = work.tile([P, BLOCKS], F32, name="inv_root")
             nc.vector.reciprocal(out=inv_root[g][:], in_=root[g][:])
 
-        def r_finish(g):
-            r_col[g] = work.tile([P, BLOCKS], F32, name="r_col")
+        def r_finish(g, c):
+            r_col[g, c] = work.tile([P, PACK], F32, name="r_col%d" % c)
+            blocks = slice(c * PACK, (c + 1) * PACK)
             nc.vector.scalar_tensor_tensor(
-                out=r_col[g][:], in0=sums[g][:], scalar=0.0, in1=inv_root[g][:], op0=ALU.is_gt, op1=ALU.mult
+                out=r_col[g, c][:],
+                in0=sums[g][:, blocks],
+                scalar=0.0,
+                in1=inv_root[g][:, blocks],
+                op0=ALU.is_gt,
+                op1=ALU.mult,
             )
 
         def r_rows(g, hf):
             r_row[g, hf] = psum.tile([P, BANK], F32, name="r_row", tag="r_row%d" % hf, bufs=1)
             for k in range(BANK // P):
-                b = hf * (BANK // P) + k
                 nc.tensor.transpose(
-                    r_row[g, hf][:, k * P : (k + 1) * P], r_col[g][:, b : b + 1].to_broadcast([P, P]), ident[:]
+                    r_row[g, hf][:, k * P : (k + 1) * P], r_col[g, hf][:, k : k + 1].to_broadcast([P, P]), ident[:]
                 )
 
         def r_row_copy(g):
@@ -238,23 +241,13 @@ def tile_gcn_pa_kernel(tc, batch_graph, adj, W1, b1, out):
             b = c * PACK + t
             dst = planes[g, c][:, t, :]
             src = adj_sb[g][:, b, :]
-            r_j = r_col[g][:, b : b + 1]
+            r_j = r_col[g, c][:, t : t + 1]
             if engine == "S":
                 nc.scalar.activation(out=dst, in_=src, func=ACT.Copy, scale=r_j)
             elif engine == "V":
                 nc.vector.tensor_scalar(out=dst, in0=src, scalar1=r_j, scalar2=None, op0=ALU.mult)
             else:
-                for half in (slice(0, BANK), slice(BANK, NODES)):
-                    nc.gpsimd.tensor_scalar(
-                        out=dst[:, half], in0=src[:, half], scalar1=r_j, scalar2=0.0, op0=ALU.mult, op1=ALU.add
-                    )
-
-        def gp_cols(g, c, hf):
-            if (c, hf) == (PASSES - 1, GPSIMD_HALF):
-                return BANK
-            if (g, c, hf) == (GRAPHS - 1, 0, GPSIMD_HALF):
-                return LAST_COLS
-            return 0
+                nc.gpsimd.tensor_scalar(out=dst, in0=src, scalar1=r_j, scalar2=0.0, op0=ALU.mult, op1=ALU.add)
 
         def a_tile(g, hf):
             if (g, hf) not in a_grouped:
@@ -262,27 +255,31 @@ def tile_gcn_pa_kernel(tc, batch_graph, adj, W1, b1, out):
 
         def a_multiply(g, c, hf):
             a_tile(g, hf)
-            w = BANK - gp_cols(g, c, hf)
             nc.vector.tensor_tensor(
-                out=a_grouped[g, hf][:, c, :w, :].rearrange("p (n i) t -> p n t i", i=RUN),
-                in0=planes[g, c][:, :, hf * BANK : hf * BANK + w].rearrange("p t (n i) -> p n t i", i=RUN),
-                in1=r_row[g, hf][:, :w]
+                out=a_grouped[g, hf][:, c, :, :].rearrange("p (n i) t -> p n t i", i=RUN),
+                in0=planes[g, c][:, :, hf * BANK : (hf + 1) * BANK].rearrange("p t (n i) -> p n t i", i=RUN),
+                in1=r_row[g, hf][:]
                 .rearrange("p (n i) -> p n i", i=RUN)
                 .unsqueeze(2)
-                .to_broadcast([P, w // RUN, PACK, RUN]),
+                .to_broadcast([P, BANK // RUN, PACK, RUN]),
                 op=ALU.mult,
             )
 
-        def a_multiply_gpsimd(g, c):
-            hf = GPSIMD_HALF
+        def gate():
+            token = work.tile([P, 1], F32, name="token")
+            taken = work.tile([P, 1], F32, name="taken")
+            nc.vector.memset(token[:], 0.0)
+            nc.gpsimd.tensor_copy(out=taken[:], in_=token[:])
+
+        def a_multiply_gpsimd(g, lo, hi):
+            c, hf = 0, GPSIMD_HALF
             a_tile(g, hf)
-            for lo in range(BANK - gp_cols(g, c, hf), BANK, GP_COLS):
-                nc.gpsimd.tensor_tensor(
-                    out=a_grouped[g, hf][:, c, lo : lo + GP_COLS, :],
-                    in0=planes[g, c][:, :, hf * BANK + lo : hf * BANK + lo + GP_COLS].rearrange("p t i -> p i t"),
-                    in1=r_row_sb[g][:, lo : lo + GP_COLS].unsqueeze(2).to_broadcast([P, GP_COLS, PACK]),
-                    op=ALU.mult,
-                )
+            nc.gpsimd.tensor_tensor(
+                out=a_grouped[g, hf][:, c, lo:hi, :],
+                in0=planes[g, c][:, :, hf * BANK + lo : hf * BANK + hi].rearrange("p t i -> p i t"),
+                in1=r_row_sb[g][:, lo:hi].unsqueeze(2).to_broadcast([P, hi - lo, PACK]),
+                op=ALU.mult,
+            )
 
         def a_quantise(g, hf):
             a_codes[g, hf] = work.tile([P, PASSES, BANK], U32, name="a_codes", bufs=4, align_bytes=64)
@@ -346,7 +343,8 @@ def tile_gcn_pa_kernel(tc, batch_graph, adj, W1, b1, out):
         h_copy(0, 1, 0, "S")
         r_invert(0)
         h_copy(0, 1, 1, "V")
-        r_finish(0)
+        r_finish(0, 0)
+        r_finish(0, 1)
         scale_plane(0, 0, 0, "S")
         scale_plane(0, 0, 1, "V")
         scale_plane(0, 0, 2, "V")
@@ -361,7 +359,6 @@ def tile_gcn_pa_kernel(tc, batch_graph, adj, W1, b1, out):
             x_transpose(1, pair)
         scale_plane(0, 1, 0, "S")
         scale_plane(0, 1, 1, "S")
-        r_row_copy(0)
         column_sums(1, 0)
         column_sums(1, 1)
 
@@ -369,74 +366,82 @@ def tile_gcn_pa_kernel(tc, batch_graph, adj, W1, b1, out):
             nxt = g + 1
             more = nxt < GRAPHS
             more2 = nxt + 1 < GRAPHS
+            if g > 0:
+                for t in range(PACK):
+                    scale_plane(g, 1, t, "SGGG"[t])
+            r_row_copy(g)
+            if g > 0:
+                a_multiply_gpsimd(g, 0, 96)
             a_multiply(g, 0, 0)
             if g == 0:
                 load_x(3)
                 load_adj(3)
             if g > 0:
+                if more:
+                    r_invert(nxt)
                 for fq in range(FQ):
                     h_copy(g, 1, fq, "S")
                 for block in range(4, 8):
                     out_add(g - 1, block)
                     out_relu(g - 1, block)
-                h_quantise(g)
-            if g == 0:
-                h_quantise(0)
-            a_multiply_gpsimd(g, 0)
-            a_multiply_gpsimd(g, 1)
+                if more:
+                    r_finish(nxt, 0)
+            h_quantise(g)
+            if not more:
+                gate()
+                a_multiply_gpsimd(g, 96, 256)
             if more:
                 if g > 0:
                     for pair in range(PAIRS):
                         x_transpose(nxt, pair)
                 for pair in range(PAIRS):
                     x_copy(nxt, pair, "S")
-            if g == 0:
-                r_sums(1)
-                r_root(1)
             if more2:
                 column_sums(nxt + 1, 0)
                 column_sums(nxt + 1, 1)
             a_multiply(g, 1, 0)
             if g == 0:
-                r_invert(1)
+                r_sums(1)
+                r_root(1)
+            if g > 0 and more:
+                for t in range(PACK):
+                    scale_plane(nxt, 0, t, "SSGG"[t])
+                r_rows(nxt, 0)
             if more:
                 x_quantise(nxt)
-            if g == 0:
-                r_finish(1)
-            if more:
-                scale_plane(nxt, 0, 0, "S")
-                scale_plane(nxt, 0, 1, "S")
-                scale_plane(nxt, 0, 2, "G")
-                scale_plane(nxt, 0, 3, "G")
-                r_rows(nxt, 0)
                 for fq in range(FQ):
                     h_matmul(nxt, 0, fq)
                     h_copy(nxt, 0, fq, "S")
+            if g == 0:
+                r_invert(1)
             if more2:
                 r_sums(nxt + 1)
-                r_root(nxt + 1)
+            gate()
             a_quantise(g, 0)
+            if g == 0:
+                r_finish(1, 0)
+                for t in range(PACK):
+                    scale_plane(1, 0, t, "SSSS"[t])
+                r_rows(1, 0)
+            if more:
+                a_multiply_gpsimd(g, 96 if g > 0 else 0, BANK)
+            else:
+                a_multiply_gpsimd(g, 256, BANK)
             for block in range(4):
                 out_matmul(g, block)
-            a_multiply(g, 0, 1)
-            if more:
-                scale_plane(nxt, 1, 0, "S")
-                scale_plane(nxt, 1, 1, "S")
-                scale_plane(nxt, 1, 2, "G")
-                scale_plane(nxt, 1, 3, "G")
-                r_rows(nxt, 1)
+            a_multiply(g, 1, 1)
             for block in range(4 if more else 2):
                 out_add(g, block)
                 out_relu(g, block)
             if more2:
-                r_invert(nxt + 1)
+                r_root(nxt + 1)
             if more:
-                r_row_copy(nxt)
                 for fq in range(FQ):
                     h_matmul(nxt, 1, fq)
             a_quantise(g, 1)
-            if more2:
-                r_finish(nxt + 1)
+            if more:
+                r_finish(nxt, 1)
+                r_rows(nxt, 1)
             for block in range(4, 8):
                 out_matmul(g, block)
         for block in range(2, 8):

@@ -31,6 +31,7 @@ FQ = F_OUT // P
 X_BUFS = 2
 PLANES_BUFS = 4
 RESULT_BUFS = 8
+A_BUFS = 2
 INPUT_BUFS = 3
 ACC_BANKS = 6
 
@@ -164,8 +165,12 @@ def tile_gcn_pa_kernel(tc, batch_graph, adj, W1, b1, out):
         def r_rows(g, hf):
             r_row[g, hf] = psum.tile([P, BANK], F32, name="r_row", tag="r_row%d" % hf, bufs=1)
             for k in range(BANK // P):
-                nc.tensor.transpose(
-                    r_row[g, hf][:, k * P : (k + 1) * P], r_col[g, hf][:, k : k + 1].to_broadcast([P, P]), ident[:]
+                nc.tensor.matmul(
+                    out=r_row[g, hf][:, k * P : (k + 1) * P],
+                    lhsT=r_col[g, hf][:, k : k + 1].to_broadcast([P, P]),
+                    rhs=ident[:],
+                    start=True,
+                    stop=True,
                 )
 
         def r_row_copy(g):
@@ -251,7 +256,7 @@ def tile_gcn_pa_kernel(tc, batch_graph, adj, W1, b1, out):
 
         def a_tile(g, hf):
             if (g, hf) not in a_grouped:
-                a_grouped[g, hf] = work.tile([P, PASSES, BANK, PACK], BF16, name="a_grouped", bufs=2, align_bytes=64)
+                a_grouped[g, hf] = work.tile([P, PASSES, BANK, PACK], BF16, name="a_grouped", bufs=A_BUFS, align_bytes=64)
 
         def a_multiply(g, c, hf):
             a_tile(g, hf)
@@ -272,7 +277,7 @@ def tile_gcn_pa_kernel(tc, batch_graph, adj, W1, b1, out):
             nc.gpsimd.tensor_copy(out=taken[:], in_=token[:])
 
         def a_multiply_gpsimd(g, lo, hi):
-            c, hf = 0, GPSIMD_HALF
+            c, hf = PASSES - 1, GPSIMD_HALF
             a_tile(g, hf)
             nc.gpsimd.tensor_tensor(
                 out=a_grouped[g, hf][:, c, lo:hi, :],
@@ -355,10 +360,12 @@ def tile_gcn_pa_kernel(tc, batch_graph, adj, W1, b1, out):
         h_copy(0, 1, 3, "S")
         scale_plane(0, 1, 2, "G")
         scale_plane(0, 1, 3, "G")
-        for pair in range(PAIRS):
+        for pair in range(3):
             x_transpose(1, pair)
         scale_plane(0, 1, 0, "S")
         scale_plane(0, 1, 1, "S")
+        for pair in range(2):
+            x_copy(1, pair, "S")
         column_sums(1, 0)
         column_sums(1, 1)
 
@@ -367,83 +374,118 @@ def tile_gcn_pa_kernel(tc, batch_graph, adj, W1, b1, out):
             more = nxt < GRAPHS
             more2 = nxt + 1 < GRAPHS
             if g > 0:
-                for t in range(PACK):
-                    scale_plane(g, 1, t, "SGGG"[t])
-            r_row_copy(g)
-            if g > 0:
-                a_multiply_gpsimd(g, 0, 96)
+                scale_plane(g, 1, 2, "G")
+                scale_plane(g, 1, 3, "G")
             a_multiply(g, 0, 0)
-            if g == 0:
+            if g > 0:
+                h_copy(g, 1, 1, "S")
+                h_copy(g, 1, 2, "S")
+            if more:
+                x_transpose(nxt, 3)
+                x_copy(nxt, 2, "S")
+            if g > 0:
+                h_matmul(g, 1, 3)
+                h_copy(g, 1, 3, "S")
+            if more:
+                x_copy(nxt, 3, "S")
+            if g > 0:
+                scale_plane(g, 1, 0, "S")
+                r_rows(g, 1)
+                r_row_copy(g)
+                out_matmul(g - 1, 4)
+                out_matmul(g - 1, 5)
+                out_add(g - 1, 3)
+                out_relu(g - 1, 0)
+            else:
+                r_row_copy(g)
                 load_x(3)
                 load_adj(3)
-            if g > 0:
-                if more:
-                    r_invert(nxt)
-                for fq in range(FQ):
-                    h_copy(g, 1, fq, "S")
-                for block in range(4, 8):
-                    out_add(g - 1, block)
-                    out_relu(g - 1, block)
-                if more:
-                    r_finish(nxt, 0)
+            if more and g > 0:
+                r_invert(nxt)
             h_quantise(g)
-            if not more:
-                gate()
-                a_multiply_gpsimd(g, 96, 256)
-            if more:
-                if g > 0:
-                    for pair in range(PAIRS):
-                        x_transpose(nxt, pair)
-                for pair in range(PAIRS):
-                    x_copy(nxt, pair, "S")
-            if more2:
-                column_sums(nxt + 1, 0)
-                column_sums(nxt + 1, 1)
-            a_multiply(g, 1, 0)
             if g == 0:
                 r_sums(1)
                 r_root(1)
-            if g > 0 and more:
-                for t in range(PACK):
-                    scale_plane(nxt, 0, t, "SSGG"[t])
-                r_rows(nxt, 0)
+            if more and g > 0:
+                r_finish(nxt, 0)
             if more:
                 x_quantise(nxt)
-                for fq in range(FQ):
-                    h_matmul(nxt, 0, fq)
-                    h_copy(nxt, 0, fq, "S")
             if g == 0:
                 r_invert(1)
+                r_finish(1, 0)
+            if more:
+                scale_plane(nxt, 0, 0, "S")
+                scale_plane(nxt, 0, 2, "G")
+                if more2:
+                    column_sums(nxt + 1, 0)
+                for fq in range(3):
+                    h_matmul(nxt, 0, fq)
+                    h_copy(nxt, 0, fq, "S")
+                if more2:
+                    column_sums(nxt + 1, 1)
+            cut = 256 if more else 384
+            a_multiply_gpsimd(g, 0, cut)
+            a_multiply_gpsimd(g, cut, BANK)
+            a_multiply(g, 1, 0)
+            if g > 0:
+                out_relu(g - 1, 1)
+                out_relu(g - 1, 2)
+                out_matmul(g - 1, 6)
+                out_matmul(g - 1, 7)
+                for block in range(4, 7):
+                    out_add(g - 1, block)
             if more2:
                 r_sums(nxt + 1)
-            gate()
-            a_quantise(g, 0)
             if g == 0:
-                r_finish(1, 0)
-                for t in range(PACK):
-                    scale_plane(1, 0, t, "SSSS"[t])
-                r_rows(1, 0)
+                a_multiply(g, 0, 1)
+            a_quantise(g, 0)
             if more:
-                a_multiply_gpsimd(g, 96 if g > 0 else 0, BANK)
-            else:
-                a_multiply_gpsimd(g, 256, BANK)
-            for block in range(4):
-                out_matmul(g, block)
-            a_multiply(g, 1, 1)
-            for block in range(4 if more else 2):
-                out_add(g, block)
-                out_relu(g, block)
+                h_matmul(nxt, 0, 3)
+                h_matmul(nxt, 1, 0)
+                h_copy(nxt, 0, 3, "S")
+            if g > 0:
+                out_relu(g - 1, 3)
+                out_relu(g - 1, 4)
+            if more:
+                scale_plane(nxt, 0, 1, "S")
+            if g > 0:
+                out_relu(g - 1, 5)
+                out_relu(g - 1, 6)
             if more2:
                 r_root(nxt + 1)
+                x_transpose(nxt + 1, 0)
+                x_copy(nxt + 1, 0, "S")
+            for block in range(3):
+                out_matmul(g, block)
+            if more2:
+                x_transpose(nxt + 1, 1)
             if more:
-                for fq in range(FQ):
-                    h_matmul(nxt, 1, fq)
-            a_quantise(g, 1)
+                r_rows(nxt, 0)
+            out_matmul(g, 3)
+            if more:
+                h_matmul(nxt, 1, 1)
+                h_matmul(nxt, 1, 2)
+                h_copy(nxt, 1, 0, "S")
+            if more2:
+                x_copy(nxt + 1, 1, "S")
+                x_transpose(nxt + 1, 2)
+            if g > 0:
+                a_multiply(g, 0, 1)
+                out_add(g - 1, 7)
+                out_relu(g - 1, 7)
+            if more:
+                scale_plane(nxt, 0, 3, "G")
+            for block in range(3):
+                out_add(g, block)
+                if not more:
+                    out_relu(g, block)
             if more:
                 r_finish(nxt, 1)
-                r_rows(nxt, 1)
-            for block in range(4, 8):
-                out_matmul(g, block)
-        for block in range(2, 8):
-            out_add(GRAPHS - 1, block)
-            out_relu(GRAPHS - 1, block)
+                scale_plane(nxt, 1, 1, "S")
+            a_quantise(g, 1)
+        last = GRAPHS - 1
+        for block in range(4, 8):
+            out_matmul(last, block)
+        for block in range(3, 8):
+            out_add(last, block)
+            out_relu(last, block)

@@ -70,12 +70,12 @@ def tile_gcn_pa_kernel(tc, batch_graph, adj, W1, b1, out):
                     out=x_sb[g][:, k * half : (k + 1) * half, :], in_=rows.rearrange("(b p) k -> p b k", p=P)
                 )
 
+        load_adj(0)
         nc.sync.dma_start(
             out=w_sb[:].rearrange("q (u e) f -> q u (e f)", u=2),
             in_=W1.rearrange("(u q e) f -> q u (e f)", u=2, e=2),
         )
         load_x(0)
-        load_adj(0)
         load_x(1)
         nc.sync.dma_start(out=bias_bf[:], in_=b1.partition_broadcast(P))
         load_adj(1)
@@ -95,7 +95,6 @@ def tile_gcn_pa_kernel(tc, batch_graph, adj, W1, b1, out):
         w_scales = consts.tile([P, F_OUT], U8, name="w_scales", align_bytes=64)
         bias = consts.tile([P, F_OUT], F32, name="bias")
 
-        colsum = {}
         sums = {}
         root = {}
         inv_root = {}
@@ -123,28 +122,21 @@ def tile_gcn_pa_kernel(tc, batch_graph, adj, W1, b1, out):
             else:
                 nc.vector.tensor_copy(out=dst, in_=bank)
 
-        def column_sums(g, c):
-            if c == 0:
-                colsum[g] = psum.tile([P, PASSES, BLOCKS, ONES_COLS], F32, name="colsum", tag="acc", bufs=ACC_BANKS)
+        def column_sums(g):
+            sums[g] = psum.tile([P, BLOCKS, ONES_COLS], F32, name="colsum", tag="acc", bufs=ACC_BANKS)
             for nb in range(BLOCKS):
-                for t in range(PACK):
+                for b in range(BLOCKS):
                     nc.tensor.matmul(
-                        out=colsum[g][:, c, nb, :],
-                        lhsT=adj_sb[g][:, c * PACK + t, nb * P : (nb + 1) * P],
+                        out=sums[g][:, nb, :],
+                        lhsT=adj_sb[g][:, b, nb * P : (nb + 1) * P],
                         rhs=ones[:],
-                        start=(t == 0),
-                        stop=(t == PACK - 1),
+                        start=(b == 0),
+                        stop=(b == BLOCKS - 1),
                     )
-
-        def r_sums(g):
-            sums[g] = work.tile([P, BLOCKS], F32, name="sums")
-            nc.vector.tensor_reduce(
-                out=sums[g][:], in_=colsum[g][:, :, :, 0].rearrange("p c b -> p b c"), axis=AXIS.X, op=ALU.add
-            )
 
         def r_root(g):
             root[g] = work.tile([P, BLOCKS], F32, name="root")
-            nc.scalar.activation(out=root[g][:], in_=sums[g][:], func=ACT.Sqrt, bias=tiny[:])
+            nc.scalar.activation(out=root[g][:], in_=sums[g][:, :, 0], func=ACT.Sqrt, bias=tiny[:])
 
         def r_invert(g):
             inv_root[g] = work.tile([P, BLOCKS], F32, name="inv_root")
@@ -155,7 +147,7 @@ def tile_gcn_pa_kernel(tc, batch_graph, adj, W1, b1, out):
             blocks = slice(c * PACK, (c + 1) * PACK)
             nc.vector.scalar_tensor_tensor(
                 out=r_col[g, c][:],
-                in0=sums[g][:, blocks],
+                in0=sums[g][:, blocks, 0],
                 scalar=0.0,
                 in1=inv_root[g][:, blocks],
                 op0=ALU.is_gt,
@@ -270,12 +262,6 @@ def tile_gcn_pa_kernel(tc, batch_graph, adj, W1, b1, out):
                 op=ALU.mult,
             )
 
-        def gate():
-            token = work.tile([P, 1], F32, name="token")
-            taken = work.tile([P, 1], F32, name="taken")
-            nc.vector.memset(token[:], 0.0)
-            nc.gpsimd.tensor_copy(out=taken[:], in_=token[:])
-
         def a_multiply_gpsimd(g, lo, hi):
             c, hf = PASSES - 1, GPSIMD_HALF
             a_tile(g, hf)
@@ -319,173 +305,180 @@ def tile_gcn_pa_kernel(tc, batch_graph, adj, W1, b1, out):
             nc.scalar.activation(out=res, in_=res, func=ACT.Relu)
             nc.sync.dma_start(out=out[g, block * P : (block + 1) * P, :], in_=res)
 
+        column_sums(0)
+        r_root(0)
         nc.vector.tensor_copy(out=w_grouped[:], in_=w_sb[:].rearrange("q t f -> q f t"))
-        for pair in range(PAIRS):
-            x_transpose(0, pair)
-        for pair in range(3):
-            x_copy(0, pair, "S")
+        r_invert(0)
+        r_finish(0, 0)
+        r_finish(0, 1)
+        for t in range(PACK):
+            scale_plane(0, 0, t, "SVVV"[t])
+        r_rows(0, 0)
         nc.vector.quantize_mx(
             out=w_codes[:].bitcast(FP8X4),
             scales=w_scales[:],
             in_=w_grouped[:].rearrange("q f t -> q (f t)"),
         )
-        x_quantise(0, 0, BANK)
-        x_copy(0, 3, "V")
+        for pair in range(PAIRS):
+            x_transpose(0, pair)
+            x_copy(0, pair, "S")
         load_x(2)
         load_adj(2)
+        for t in range(PACK):
+            scale_plane(0, 1, t, "SSGG"[t])
+        r_rows(0, 1)
+        r_row_copy(0)
+        a_multiply(0, 0, 0)
+        x_quantise(0)
+        nc.vector.tensor_copy(out=bias[:], in_=bias_bf[:])
         for fq in range(FQ):
             h_matmul(0, 0, fq)
-        x_quantise(0, BANK, NODES)
-        for fq in range(FQ):
-            h_copy(0, 0, fq, "SV"[fq % 2])
-        column_sums(0, 0)
-        column_sums(0, 1)
-        for fq in range(FQ):
-            h_matmul(0, 1, fq)
-        r_sums(0)
-        r_root(0)
-        nc.vector.tensor_copy(out=bias[:], in_=bias_bf[:])
+        for fq in range(3):
+            h_copy(0, 0, fq, "S")
+        h_matmul(0, 1, 0)
         h_copy(0, 1, 0, "S")
-        r_invert(0)
-        h_copy(0, 1, 1, "V")
-        r_finish(0, 0)
-        r_finish(0, 1)
-        scale_plane(0, 0, 0, "S")
-        scale_plane(0, 0, 1, "V")
-        scale_plane(0, 0, 2, "V")
-        scale_plane(0, 0, 3, "V")
-        r_rows(0, 0)
-        r_rows(0, 1)
-        h_copy(0, 1, 2, "S")
-        h_copy(0, 1, 3, "S")
-        scale_plane(0, 1, 2, "G")
-        scale_plane(0, 1, 3, "G")
-        for pair in range(3):
-            x_transpose(1, pair)
-        scale_plane(0, 1, 0, "S")
-        scale_plane(0, 1, 1, "S")
-        for pair in range(2):
-            x_copy(1, pair, "S")
-        column_sums(1, 0)
-        column_sums(1, 1)
 
-        for g in range(GRAPHS):
+        a_multiply_gpsimd(0, 0, BANK // 2)
+        a_multiply_gpsimd(0, BANK // 2, BANK)
+        a_multiply(0, 1, 0)
+        for fq in range(3, FQ):
+            h_copy(0, 0, fq, "S")
+        for fq in range(1, FQ):
+            h_matmul(0, 1, fq)
+            h_copy(0, 1, fq, "S")
+        column_sums(1)
+        for pair in range(2):
+            x_transpose(1, pair)
+        for pair in range(2, PAIRS):
+            x_transpose(1, pair)
+        a_multiply(0, 0, 1)
+        r_root(1)
+        load_x(3)
+        load_adj(3)
+        for pair in range(PAIRS):
+            x_copy(1, pair, "S")
+        a_quantise(0, 0)
+        h_quantise(0)
+        for block in range(3):
+            out_matmul(0, block)
+        r_invert(1)
+        r_finish(1, 0)
+        r_finish(1, 1)
+        for t in range(PACK):
+            scale_plane(1, 0, t, "SSGG"[t])
+        r_rows(1, 0)
+        x_quantise(1)
+        for block in range(3):
+            out_add(0, block)
+        for fq in range(3):
+            h_matmul(1, 0, fq)
+            h_copy(1, 0, fq, "S")
+        out_matmul(0, 3)
+        h_matmul(1, 0, 3)
+        r_rows(1, 1)
+        h_matmul(1, 1, 0)
+        scale_plane(1, 1, 1, "S")
+        h_copy(1, 1, 0, "S")
+        scale_plane(1, 1, 0, "S")
+        a_quantise(0, 1)
+        out_add(0, 3)
+
+        for g in range(1, GRAPHS):
             nxt = g + 1
             more = nxt < GRAPHS
-            more2 = nxt + 1 < GRAPHS
-            if g > 0:
-                scale_plane(g, 1, 2, "G")
-                scale_plane(g, 1, 3, "G")
+            if more:
+                column_sums(nxt)
+            scale_plane(g, 1, 2, "G")
+            scale_plane(g, 1, 3, "G")
             a_multiply(g, 0, 0)
-            if g > 0:
-                h_copy(g, 1, 1, "S")
-                h_copy(g, 1, 2, "S")
+            out_matmul(g - 1, 4)
+            out_matmul(g - 1, 5)
+            out_add(g - 1, 4)
+            if g >= 2:
+                out_relu(g - 2, 6)
+            h_copy(g, 0, 3, "S")
+            r_row_copy(g)
+            if g >= 2:
+                out_relu(g - 2, 7)
             if more:
-                x_transpose(nxt, 3)
-                x_copy(nxt, 2, "S")
-            if g > 0:
-                h_matmul(g, 1, 3)
-                h_copy(g, 1, 3, "S")
+                r_root(nxt)
+            h_matmul(g, 1, 1)
+            h_matmul(g, 1, 2)
             if more:
-                x_copy(nxt, 3, "S")
-            if g > 0:
-                scale_plane(g, 1, 0, "S")
-                r_rows(g, 1)
-                r_row_copy(g)
-                out_matmul(g - 1, 4)
-                out_matmul(g - 1, 5)
-                out_add(g - 1, 3)
-                out_relu(g - 1, 0)
-            else:
-                r_row_copy(g)
-                load_x(3)
-                load_adj(3)
-            if more and g > 0:
-                r_invert(nxt)
-            h_quantise(g)
-            if g == 0:
-                r_sums(1)
-                r_root(1)
-            if more and g > 0:
-                r_finish(nxt, 0)
+                for pair in range(2):
+                    x_transpose(nxt, pair)
+                    x_copy(nxt, pair, "S")
+            h_copy(g, 1, 1, "S")
+            out_relu(g - 1, 0)
             if more:
-                x_quantise(nxt)
-            if g == 0:
-                r_invert(1)
-                r_finish(1, 0)
-            if more:
-                scale_plane(nxt, 0, 0, "S")
-                scale_plane(nxt, 0, 2, "G")
-                if more2:
-                    column_sums(nxt + 1, 0)
-                for fq in range(3):
-                    h_matmul(nxt, 0, fq)
-                    h_copy(nxt, 0, fq, "S")
-                if more2:
-                    column_sums(nxt + 1, 1)
-            cut = 256 if more else 384
-            a_multiply_gpsimd(g, 0, cut)
-            a_multiply_gpsimd(g, cut, BANK)
+                for pair in range(2, PAIRS):
+                    x_transpose(nxt, pair)
+                    x_copy(nxt, pair, "S")
+            h_matmul(g, 1, 3)
+            h_copy(g, 1, 2, "S")
+            h_copy(g, 1, 3, "S")
+            a_multiply_gpsimd(g, 0, BANK // 2)
             a_multiply(g, 1, 0)
-            if g > 0:
-                out_relu(g - 1, 1)
-                out_relu(g - 1, 2)
-                out_matmul(g - 1, 6)
-                out_matmul(g - 1, 7)
-                for block in range(4, 7):
-                    out_add(g - 1, block)
-            if more2:
-                r_sums(nxt + 1)
-            if g == 0:
-                a_multiply(g, 0, 1)
+            if more:
+                r_invert(nxt)
+            out_matmul(g - 1, 6)
+            out_matmul(g - 1, 7)
+            out_add(g - 1, 5)
+            if more:
+                r_finish(nxt, 0)
+                r_rows(nxt, 0)
             a_quantise(g, 0)
             if more:
-                h_matmul(nxt, 0, 3)
-                h_matmul(nxt, 1, 0)
-                h_copy(nxt, 0, 3, "S")
-            if g > 0:
-                out_relu(g - 1, 3)
-                out_relu(g - 1, 4)
+                x_quantise(nxt)
+            h_quantise(g)
             if more:
-                scale_plane(nxt, 0, 1, "S")
-            if g > 0:
-                out_relu(g - 1, 5)
-                out_relu(g - 1, 6)
-            if more2:
-                r_root(nxt + 1)
-                x_transpose(nxt + 1, 0)
-                x_copy(nxt + 1, 0, "S")
+                h_matmul(nxt, 0, 0)
+                h_matmul(nxt, 0, 1)
+                scale_plane(nxt, 0, 2, "G")
+            a_multiply_gpsimd(g, BANK // 2, BANK)
             for block in range(3):
                 out_matmul(g, block)
-            if more2:
-                x_transpose(nxt + 1, 1)
+            out_relu(g - 1, 1)
             if more:
-                r_rows(nxt, 0)
+                scale_plane(nxt, 0, 0, "S")
+            out_relu(g - 1, 2)
+            out_relu(g - 1, 3)
+            out_add(g - 1, 6)
+            out_add(g - 1, 7)
+            if more:
+                r_finish(nxt, 1)
+                h_matmul(nxt, 0, 2)
             out_matmul(g, 3)
             if more:
-                h_matmul(nxt, 1, 1)
-                h_matmul(nxt, 1, 2)
-                h_copy(nxt, 1, 0, "S")
-            if more2:
-                x_copy(nxt + 1, 1, "S")
-                x_transpose(nxt + 1, 2)
-            if g > 0:
-                a_multiply(g, 0, 1)
-                out_add(g - 1, 7)
-                out_relu(g - 1, 7)
-            if more:
+                h_copy(nxt, 0, 0, "S")
+                h_matmul(nxt, 0, 3)
+                scale_plane(nxt, 0, 1, "S")
                 scale_plane(nxt, 0, 3, "G")
+                h_copy(nxt, 0, 1, "S")
+                h_copy(nxt, 0, 2, "S")
+            a_multiply(g, 0, 1)
+            out_relu(g - 1, 4)
+            if more:
+                r_rows(nxt, 1)
+                h_matmul(nxt, 1, 0)
+                scale_plane(nxt, 1, 1, "S")
+                h_copy(nxt, 1, 0, "S")
+            out_relu(g - 1, 5)
+            if more:
+                scale_plane(nxt, 1, 0, "S")
             for block in range(3):
                 out_add(g, block)
                 if not more:
                     out_relu(g, block)
-            if more:
-                r_finish(nxt, 1)
-                scale_plane(nxt, 1, 1, "S")
             a_quantise(g, 1)
+            out_add(g, 3)
+            if not more:
+                out_relu(g, 3)
         last = GRAPHS - 1
         for block in range(4, 8):
             out_matmul(last, block)
-        for block in range(3, 8):
+        out_relu(last - 1, 6)
+        out_relu(last - 1, 7)
+        for block in range(4, 8):
             out_add(last, block)
             out_relu(last, block)

@@ -63,12 +63,7 @@ def tile_gcn_pa_kernel(tc, batch_graph, adj, W1, b1, out):
 
         def load_x(g):
             x_sb[g] = inputs.tile([P, BLOCKS, F_IN], BF16, name="x_sb", tag="x_sb", bufs=X_BUFS)
-            half = BLOCKS // 2
-            for k in range(2):
-                rows = batch_graph[g, k * half * P : (k + 1) * half * P, :]
-                nc.sync.dma_start(
-                    out=x_sb[g][:, k * half : (k + 1) * half, :], in_=rows.rearrange("(b p) k -> p b k", p=P)
-                )
+            nc.sync.dma_start(out=x_sb[g][:], in_=batch_graph[g].rearrange("(b p) k -> p b k", p=P))
 
         load_adj(0)
         nc.sync.dma_start(
@@ -93,7 +88,6 @@ def tile_gcn_pa_kernel(tc, batch_graph, adj, W1, b1, out):
         w_grouped = consts.tile([P, F_OUT, PACK], BF16, name="w_grouped", align_bytes=64)
         w_codes = consts.tile([P, F_OUT], U32, name="w_codes", align_bytes=64)
         w_scales = consts.tile([P, F_OUT], U8, name="w_scales", align_bytes=64)
-        bias = consts.tile([P, F_OUT], F32, name="bias")
 
         sums = {}
         root = {}
@@ -250,20 +244,26 @@ def tile_gcn_pa_kernel(tc, batch_graph, adj, W1, b1, out):
             if (g, hf) not in a_grouped:
                 a_grouped[g, hf] = work.tile([P, PASSES, BANK, PACK], BF16, name="a_grouped", bufs=A_BUFS, align_bytes=64)
 
-        def a_multiply(g, c, hf):
+        def a_multiply(g, c, hf, lo=0, hi=BANK):
             a_tile(g, hf)
             nc.vector.tensor_tensor(
-                out=a_grouped[g, hf][:, c, :, :].rearrange("p (n i) t -> p n t i", i=RUN),
-                in0=planes[g, c][:, :, hf * BANK : (hf + 1) * BANK].rearrange("p t (n i) -> p n t i", i=RUN),
-                in1=r_row[g, hf][:]
+                out=a_grouped[g, hf][:, c, lo:hi, :].rearrange("p (n i) t -> p n t i", i=RUN),
+                in0=planes[g, c][:, :, hf * BANK + lo : hf * BANK + hi].rearrange("p t (n i) -> p n t i", i=RUN),
+                in1=r_row[g, hf][:, lo:hi]
                 .rearrange("p (n i) -> p n i", i=RUN)
                 .unsqueeze(2)
-                .to_broadcast([P, BANK // RUN, PACK, RUN]),
+                .to_broadcast([P, (hi - lo) // RUN, PACK, RUN]),
                 op=ALU.mult,
             )
 
-        def a_multiply_gpsimd(g, lo, hi):
-            c, hf = PASSES - 1, GPSIMD_HALF
+        def gate():
+            token = work.tile([P, 1], F32, name="token")
+            taken = work.tile([P, 1], F32, name="taken")
+            nc.vector.memset(token[:], 0.0)
+            nc.gpsimd.tensor_copy(out=taken[:], in_=token[:])
+
+        def a_multiply_gpsimd(g, lo, hi, c=PASSES - 1):
+            hf = GPSIMD_HALF
             a_tile(g, hf)
             nc.gpsimd.tensor_tensor(
                 out=a_grouped[g, hf][:, c, lo:hi, :],
@@ -298,7 +298,7 @@ def tile_gcn_pa_kernel(tc, batch_graph, adj, W1, b1, out):
 
         def out_add(g, block):
             result[g, block] = work.tile([P, F_OUT], F32, name="result", bufs=RESULT_BUFS)
-            nc.vector.tensor_tensor(out=result[g, block][:], in0=out_acc[g, block][:], in1=bias[:], op=ALU.add)
+            nc.vector.tensor_tensor(out=result[g, block][:], in0=out_acc[g, block][:], in1=bias_bf[:], op=ALU.add)
 
         def out_relu(g, block):
             res = result[g, block][:]
@@ -330,7 +330,6 @@ def tile_gcn_pa_kernel(tc, batch_graph, adj, W1, b1, out):
         r_row_copy(0)
         a_multiply(0, 0, 0)
         x_quantise(0)
-        nc.vector.tensor_copy(out=bias[:], in_=bias_bf[:])
         for fq in range(FQ):
             h_matmul(0, 0, fq)
         for fq in range(3):
@@ -338,8 +337,7 @@ def tile_gcn_pa_kernel(tc, batch_graph, adj, W1, b1, out):
         h_matmul(0, 1, 0)
         h_copy(0, 1, 0, "S")
 
-        a_multiply_gpsimd(0, 0, BANK // 2)
-        a_multiply_gpsimd(0, BANK // 2, BANK)
+        a_multiply_gpsimd(0, 0, 448)
         a_multiply(0, 1, 0)
         for fq in range(3, FQ):
             h_copy(0, 0, fq, "S")
@@ -352,6 +350,7 @@ def tile_gcn_pa_kernel(tc, batch_graph, adj, W1, b1, out):
         for pair in range(2, PAIRS):
             x_transpose(1, pair)
         a_multiply(0, 0, 1)
+        a_multiply(0, 1, 1, 448, BANK)
         r_root(1)
         load_x(3)
         load_adj(3)
@@ -436,6 +435,8 @@ def tile_gcn_pa_kernel(tc, batch_graph, adj, W1, b1, out):
                 h_matmul(nxt, 0, 1)
                 scale_plane(nxt, 0, 2, "G")
             a_multiply_gpsimd(g, BANK // 2, BANK)
+            if not more:
+                a_multiply_gpsimd(g, 384, BANK, c=0)
             for block in range(3):
                 out_matmul(g, block)
             out_relu(g - 1, 1)
@@ -456,7 +457,7 @@ def tile_gcn_pa_kernel(tc, batch_graph, adj, W1, b1, out):
                 scale_plane(nxt, 0, 3, "G")
                 h_copy(nxt, 0, 1, "S")
                 h_copy(nxt, 0, 2, "S")
-            a_multiply(g, 0, 1)
+            a_multiply(g, 0, 1, 0, BANK if more else 384)
             out_relu(g - 1, 4)
             if more:
                 r_rows(nxt, 1)
@@ -466,19 +467,18 @@ def tile_gcn_pa_kernel(tc, batch_graph, adj, W1, b1, out):
             out_relu(g - 1, 5)
             if more:
                 scale_plane(nxt, 1, 0, "S")
-            for block in range(3):
+            for block in range(3 if more else 2):
                 out_add(g, block)
                 if not more:
                     out_relu(g, block)
             a_quantise(g, 1)
-            out_add(g, 3)
-            if not more:
-                out_relu(g, 3)
+            if more:
+                out_add(g, 3)
         last = GRAPHS - 1
         for block in range(4, 8):
             out_matmul(last, block)
         out_relu(last - 1, 6)
         out_relu(last - 1, 7)
-        for block in range(4, 8):
+        for block in range(2, 8):
             out_add(last, block)
             out_relu(last, block)

from contextlib import ExitStack

import concourse.mybir as mybir
from concourse.masks import make_identity

F32 = mybir.dt.float32
BF16 = mybir.dt.bfloat16
U32 = mybir.dt.uint32
U8 = mybir.dt.uint8
FP8X4 = mybir.dt.float8_e4m3fn_x4
ALU = mybir.AluOpType
ACT = mybir.ActivationFunctionType
AXIS = mybir.AxisListType

P = 128
PACK = 4
GRAPHS = 4
NODES = 1024
F_IN = 512
F_OUT = 512
BLOCKS = NODES // P
PASSES = NODES // (P * PACK)
BANK = 512
HALVES = NODES // BANK
ONES_COLS = 32
TINY = 2.0**-126
RUN = 4
GPSIMD_HALF = 1
PAIRS = BLOCKS // 2
FQ = F_OUT // P
X_BUFS = 2
PLANES_BUFS = 4
RESULT_BUFS = 8
A_BUFS = 2
INPUT_BUFS = 3
ACC_BANKS = 6

FLOPS = 2 * GRAPHS * NODES * F_IN * F_OUT + 2 * GRAPHS * NODES * NODES * F_OUT


def tile_gcn_pa_kernel(tc, batch_graph, adj, W1, b1, out):
    nc = tc.nc
    with ExitStack() as ctx:
        ctx.enter_context(tc.manual_schedule())
        consts = ctx.enter_context(tc.tile_pool(name="consts", bufs=1))
        inputs = ctx.enter_context(tc.tile_pool(name="inputs", bufs=INPUT_BUFS))
        work = ctx.enter_context(tc.tile_pool(name="work", bufs=2))
        psum = ctx.enter_context(tc.psum_pool(name="psum", bufs=2))

        adj_sb = {}
        x_sb = {}
        w_sb = consts.tile([P, PACK, F_OUT], BF16, name="w_sb")
        bias_bf = consts.tile([P, F_OUT], BF16, name="bias_bf")

        def load_adj(g):
            adj_sb[g] = inputs.tile([P, BLOCKS, NODES], BF16, name="adj_sb", tag="adj_sb", bufs=INPUT_BUFS)
            for c in range(PASSES):
                rows = adj[g, c * P * PACK : (c + 1) * P * PACK, :]
                nc.sync.dma_start(
                    out=adj_sb[g][:, c * PACK : (c + 1) * PACK, :],
                    in_=rows.rearrange("(t p) i -> p t i", p=P),
                )

        def load_x(g):
            x_sb[g] = inputs.tile([P, BLOCKS, F_IN], BF16, name="x_sb", tag="x_sb", bufs=X_BUFS)
            nc.sync.dma_start(out=x_sb[g][:], in_=batch_graph[g].rearrange("(b p) k -> p b k", p=P))

        load_adj(0)
        nc.sync.dma_start(
            out=w_sb[:].rearrange("q (u e) f -> q u (e f)", u=2),
            in_=W1.rearrange("(u q e) f -> q u (e f)", u=2, e=2),
        )
        load_x(0)
        load_x(1)
        nc.sync.dma_start(out=bias_bf[:], in_=b1.partition_broadcast(P))
        load_adj(1)

        warm = consts.tile([P, 1], F32, name="warm")
        nc.vector.memset(warm[:], 1.0)
        nc.scalar.sqrt(out=warm[:], in_=warm[:])
        tiny = consts.tile([P, 1], F32, name="tiny")
        nc.vector.memset(tiny[:], TINY)
        ones = consts.tile([P, ONES_COLS], BF16, name="ones")
        nc.vector.memset(ones[:], 1.0)
        ident = consts.tile([P, P], F32, name="ident")
        make_identity(nc, ident[:])

        w_grouped = consts.tile([P, F_OUT, PACK], BF16, name="w_grouped", align_bytes=64)
        w_codes = consts.tile([P, F_OUT], U32, name="w_codes", align_bytes=64)
        w_scales = consts.tile([P, F_OUT], U8, name="w_scales", align_bytes=64)

        sums = {}
        root = {}
        inv_root = {}
        r_col = {}
        r_row = {}
        r_row_sb = {}
        x_grouped = {}
        x_turned = {}
        h_acc = {}
        x_codes = {}
        x_scales = {}
        h_grouped = {}
        h_codes = {}
        h_scales = {}
        planes = {}
        a_grouped = {}
        a_codes = {}
        a_scales = {}
        out_acc = {}
        result = {}

        def copy_out(engine, dst, bank):
            if engine == "S":
                nc.scalar.copy(out=dst, in_=bank)
            else:
                nc.vector.tensor_copy(out=dst, in_=bank)

        def column_sums(g):
            sums[g] = psum.tile([P, BLOCKS, ONES_COLS], F32, name="colsum", tag="acc", bufs=ACC_BANKS)
            for nb in range(BLOCKS):
                for b in range(BLOCKS):
                    nc.tensor.matmul(
                        out=sums[g][:, nb, :],
                        lhsT=adj_sb[g][:, b, nb * P : (nb + 1) * P],
                        rhs=ones[:],
                        start=(b == 0),
                        stop=(b == BLOCKS - 1),
                    )

        def r_root(g):
            root[g] = work.tile([P, BLOCKS], F32, name="root")
            nc.scalar.activation(out=root[g][:], in_=sums[g][:, :, 0], func=ACT.Sqrt, bias=tiny[:])

        def r_invert(g):
            inv_root[g] = work.tile([P, BLOCKS], F32, name="inv_root")
            nc.vector.reciprocal(out=inv_root[g][:], in_=root[g][:])

        def r_finish(g, c):
            r_col[g, c] = work.tile([P, PACK], F32, name="r_col%d" % c)
            blocks = slice(c * PACK, (c + 1) * PACK)
            nc.vector.scalar_tensor_tensor(
                out=r_col[g, c][:],
                in0=sums[g][:, blocks, 0],
                scalar=0.0,
                in1=inv_root[g][:, blocks],
                op0=ALU.is_gt,
                op1=ALU.mult,
            )

        def r_rows(g, hf):
            r_row[g, hf] = psum.tile([P, BANK], F32, name="r_row", tag="r_row%d" % hf, bufs=1)
            for k in range(BANK // P):
                nc.tensor.matmul(
                    out=r_row[g, hf][:, k * P : (k + 1) * P],
                    lhsT=r_col[g, hf][:, k : k + 1].to_broadcast([P, P]),
                    rhs=ident[:],
                    start=True,
                    stop=True,
                )

        def r_row_copy(g):
            r_row_sb[g] = work.tile([P, BANK], F32, name="r_row_sb")
            nc.scalar.copy(out=r_row_sb[g][:], in_=r_row[g, GPSIMD_HALF][:])

        def x_transpose(g, pair):
            if pair == 0:
                x_grouped[g] = work.tile([P, NODES * PACK], BF16, name="x_grouped", bufs=1, align_bytes=64)
            x_t = psum.tile([P, 2, 2, P], F32, name="x_t", tag="acc", bufs=ACC_BANKS)
            for i in range(2):
                words = x_sb[g][:, 2 * pair + i, :].bitcast(F32)
                for u in range(2):
                    nc.tensor.transpose(x_t[:, i, u, :], words[:, u * P : (u + 1) * P], ident[:])
            x_turned[g, pair] = x_t

        def x_copy(g, pair, engine):
            x_words = x_grouped[g][:].bitcast(F32).rearrange("q (n u) -> q n u", u=2)
            copy_out(
                engine,
                x_words[:, pair * 2 * P : (pair + 1) * 2 * P, :].rearrange("q (i n) u -> q i n u", i=2),
                x_turned[g, pair][:].rearrange("q i u n -> q i n u"),
            )

        def x_quantise(g, lo=0, hi=NODES):
            if lo == 0:
                x_codes[g] = work.tile([P, NODES], U32, name="x_codes", bufs=1, align_bytes=64)
                x_scales[g] = work.tile([P, NODES], U8, name="x_scales", bufs=1, align_bytes=64)
            nodes = slice(lo, hi)
            nc.vector.quantize_mx(
                out=x_codes[g][:, nodes].bitcast(FP8X4),
                scales=x_scales[g][:, nodes],
                in_=x_grouped[g][:, lo * PACK : hi * PACK],
            )

        def h_matmul(g, c, fq):
            if (c, fq) == (0, 0):
                h_grouped[g] = work.tile([P, PASSES, F_OUT, PACK], BF16, name="h_grouped", bufs=1, align_bytes=64)
            f_cols = slice(fq * P, (fq + 1) * P)
            h_acc[g, c, fq] = psum.tile([P, PACK, P], F32, name="h_acc", tag="acc", bufs=ACC_BANKS)
            for t in range(PACK):
                n_cols = slice((c * PACK + t) * P, (c * PACK + t + 1) * P)
                nc.tensor.matmul_mx(
                    out=h_acc[g, c, fq][:, t, :],
                    lhsT=x_codes[g][:, n_cols].bitcast(FP8X4),
                    lhsT_scale=x_scales[g][:, n_cols],
                    rhs=w_codes[:, f_cols].bitcast(FP8X4),
                    rhs_scale=w_scales[:, f_cols],
                    start=True,
                    stop=True,
                )

        def h_copy(g, c, fq, engine):
            copy_out(
                engine,
                h_grouped[g][:, c, fq * P : (fq + 1) * P, :],
                h_acc[g, c, fq][:].rearrange("p t f -> p f t"),
            )

        def h_quantise(g):
            if True:
                h_codes[g] = work.tile([P, PASSES, F_OUT], U32, name="h_codes", align_bytes=64)
                h_scales[g] = work.tile([P, PASSES, F_OUT], U8, name="h_scales", align_bytes=64)
            nc.vector.quantize_mx(
                out=h_codes[g][:].rearrange("p c f -> p (c f)").bitcast(FP8X4),
                scales=h_scales[g][:].rearrange("p c f -> p (c f)"),
                in_=h_grouped[g][:].rearrange("p c f t -> p (c f t)"),
            )

        def scale_plane(g, c, t, engine):
            if (g, c) not in planes:
                planes[g, c] = work.tile([P, PACK, NODES], F32, name="planes", bufs=PLANES_BUFS)
            b = c * PACK + t
            dst = planes[g, c][:, t, :]
            src = adj_sb[g][:, b, :]
            r_j = r_col[g, c][:, t : t + 1]
            if engine == "S":
                nc.scalar.activation(out=dst, in_=src, func=ACT.Copy, scale=r_j)
            elif engine == "V":
                nc.vector.tensor_scalar(out=dst, in0=src, scalar1=r_j, scalar2=None, op0=ALU.mult)
            else:
                nc.gpsimd.tensor_scalar(out=dst, in0=src, scalar1=r_j, scalar2=0.0, op0=ALU.mult, op1=ALU.add)

        def a_tile(g, hf):
            if (g, hf) not in a_grouped:
                a_grouped[g, hf] = work.tile([P, PASSES, BANK, PACK], BF16, name="a_grouped", bufs=A_BUFS, align_bytes=64)

        def a_multiply(g, c, hf, lo=0, hi=BANK):
            a_tile(g, hf)
            nc.vector.tensor_tensor(
                out=a_grouped[g, hf][:, c, lo:hi, :].rearrange("p (n i) t -> p n t i", i=RUN),
                in0=planes[g, c][:, :, hf * BANK + lo : hf * BANK + hi].rearrange("p t (n i) -> p n t i", i=RUN),
                in1=r_row[g, hf][:, lo:hi]
                .rearrange("p (n i) -> p n i", i=RUN)
                .unsqueeze(2)
                .to_broadcast([P, (hi - lo) // RUN, PACK, RUN]),
                op=ALU.mult,
            )

        def gate():
            token = work.tile([P, 1], F32, name="token")
            taken = work.tile([P, 1], F32, name="taken")
            nc.vector.memset(token[:], 0.0)
            nc.gpsimd.tensor_copy(out=taken[:], in_=token[:])

        def a_multiply_gpsimd(g, lo, hi, c=PASSES - 1):
            hf = GPSIMD_HALF
            a_tile(g, hf)
            nc.gpsimd.tensor_tensor(
                out=a_grouped[g, hf][:, c, lo:hi, :],
                in0=planes[g, c][:, :, hf * BANK + lo : hf * BANK + hi].rearrange("p t i -> p i t"),
                in1=r_row_sb[g][:, lo:hi].unsqueeze(2).to_broadcast([P, hi - lo, PACK]),
                op=ALU.mult,
            )

        def a_quantise(g, hf):
            a_codes[g, hf] = work.tile([P, PASSES, BANK], U32, name="a_codes", bufs=4, align_bytes=64)
            a_scales[g, hf] = work.tile([P, PASSES, BANK], U8, name="a_scales", bufs=4, align_bytes=64)
            nc.vector.quantize_mx(
                out=a_codes[g, hf][:].rearrange("p c i -> p (c i)").bitcast(FP8X4),
                scales=a_scales[g, hf][:].rearrange("p c i -> p (c i)"),
                in_=a_grouped[g, hf][:].rearrange("p c i t -> p (c i t)"),
            )

        def out_matmul(g, block):
            hf, k = divmod(block, BANK // P)
            i_cols = slice(k * P, (k + 1) * P)
            out_acc[g, block] = psum.tile([P, F_OUT], F32, name="out_acc", tag="acc", bufs=ACC_BANKS)
            for c in range(PASSES):
                nc.tensor.matmul_mx(
                    out=out_acc[g, block][:],
                    lhsT=a_codes[g, hf][:, c, i_cols].bitcast(FP8X4),
                    lhsT_scale=a_scales[g, hf][:, c, i_cols],
                    rhs=h_codes[g][:, c, :].bitcast(FP8X4),
                    rhs_scale=h_scales[g][:, c, :],
                    start=(c == 0),
                    stop=(c == PASSES - 1),
                )

        def out_add(g, block):
            result[g, block] = work.tile([P, F_OUT], F32, name="result", bufs=RESULT_BUFS)
            nc.vector.tensor_tensor(out=result[g, block][:], in0=out_acc[g, block][:], in1=bias_bf[:], op=ALU.add)

        def out_relu(g, block):
            res = result[g, block][:]
            nc.scalar.activation(out=res, in_=res, func=ACT.Relu)
            nc.sync.dma_start(out=out[g, block * P : (block + 1) * P, :], in_=res)

        column_sums(0)
        r_root(0)
        nc.vector.tensor_copy(out=w_grouped[:], in_=w_sb[:].rearrange("q t f -> q f t"))
        r_invert(0)
        r_finish(0, 0)
        r_finish(0, 1)
        for t in range(PACK):
            scale_plane(0, 0, t, "SVVV"[t])
        r_rows(0, 0)
        nc.vector.quantize_mx(
            out=w_codes[:].bitcast(FP8X4),
            scales=w_scales[:],
            in_=w_grouped[:].rearrange("q f t -> q (f t)"),
        )
        for pair in range(PAIRS):
            x_transpose(0, pair)
            x_copy(0, pair, "S")
        load_x(2)
        load_adj(2)
        for t in range(PACK):
            scale_plane(0, 1, t, "SSGG"[t])
        r_rows(0, 1)
        r_row_copy(0)
        a_multiply(0, 0, 0)
        x_quantise(0)
        for fq in range(FQ):
            h_matmul(0, 0, fq)
        for fq in range(3):
            h_copy(0, 0, fq, "S")
        h_matmul(0, 1, 0)
        h_copy(0, 1, 0, "S")

        a_multiply_gpsimd(0, 0, 448)
        a_multiply(0, 1, 0)
        for fq in range(3, FQ):
            h_copy(0, 0, fq, "S")
        for fq in range(1, FQ):
            h_matmul(0, 1, fq)
            h_copy(0, 1, fq, "S")
        column_sums(1)
        for pair in range(2):
            x_transpose(1, pair)
        for pair in range(2, PAIRS):
            x_transpose(1, pair)
        a_multiply(0, 0, 1)
        a_multiply(0, 1, 1, 448, BANK)
        r_root(1)
        load_x(3)
        load_adj(3)
        for pair in range(PAIRS):
            x_copy(1, pair, "S")
        a_quantise(0, 0)
        h_quantise(0)
        for block in range(3):
            out_matmul(0, block)
        r_invert(1)
        r_finish(1, 0)
        r_finish(1, 1)
        for t in range(PACK):
            scale_plane(1, 0, t, "SSGG"[t])
        r_rows(1, 0)
        x_quantise(1)
        for block in range(3):
            out_add(0, block)
        for fq in range(3):
            h_matmul(1, 0, fq)
            h_copy(1, 0, fq, "S")
        out_matmul(0, 3)
        h_matmul(1, 0, 3)
        r_rows(1, 1)
        h_matmul(1, 1, 0)
        scale_plane(1, 1, 1, "S")
        h_copy(1, 1, 0, "S")
        scale_plane(1, 1, 0, "S")
        a_quantise(0, 1)
        out_add(0, 3)

        for g in range(1, GRAPHS):
            nxt = g + 1
            more = nxt < GRAPHS
            if more:
                column_sums(nxt)
            scale_plane(g, 1, 2, "G")
            scale_plane(g, 1, 3, "G")
            a_multiply(g, 0, 0)
            out_matmul(g - 1, 4)
            out_matmul(g - 1, 5)
            out_add(g - 1, 4)
            if g >= 2:
                out_relu(g - 2, 6)
            h_copy(g, 0, 3, "S")
            r_row_copy(g)
            if g >= 2:
                out_relu(g - 2, 7)
            if more:
                r_root(nxt)
            h_matmul(g, 1, 1)
            h_matmul(g, 1, 2)
            if more:
                for pair in range(2):
                    x_transpose(nxt, pair)
                    x_copy(nxt, pair, "S")
            h_copy(g, 1, 1, "S")
            out_relu(g - 1, 0)
            if more:
                for pair in range(2, PAIRS):
                    x_transpose(nxt, pair)
                    x_copy(nxt, pair, "S")
            h_matmul(g, 1, 3)
            h_copy(g, 1, 2, "S")
            h_copy(g, 1, 3, "S")
            a_multiply_gpsimd(g, 0, BANK // 2)
            a_multiply(g, 1, 0)
            if more:
                r_invert(nxt)
            out_matmul(g - 1, 6)
            out_matmul(g - 1, 7)
            out_add(g - 1, 5)
            if more:
                r_finish(nxt, 0)
                r_rows(nxt, 0)
            a_quantise(g, 0)
            if more:
                x_quantise(nxt)
            h_quantise(g)
            if more:
                h_matmul(nxt, 0, 0)
                h_matmul(nxt, 0, 1)
                scale_plane(nxt, 0, 2, "G")
            a_multiply_gpsimd(g, BANK // 2, BANK)
            if not more:
                a_multiply_gpsimd(g, 384, BANK, c=0)
            for block in range(3):
                out_matmul(g, block)
            out_relu(g - 1, 1)
            if more:
                scale_plane(nxt, 0, 0, "S")
            out_relu(g - 1, 2)
            out_relu(g - 1, 3)
            out_add(g - 1, 6)
            out_add(g - 1, 7)
            if more:
                r_finish(nxt, 1)
                h_matmul(nxt, 0, 2)
            out_matmul(g, 3)
            if more:
                h_copy(nxt, 0, 0, "S")
                h_matmul(nxt, 0, 3)
                scale_plane(nxt, 0, 1, "S")
                scale_plane(nxt, 0, 3, "G")
                h_copy(nxt, 0, 1, "S")
                h_copy(nxt, 0, 2, "S")
            a_multiply(g, 0, 1, 0, BANK if more else 384)
            out_relu(g - 1, 4)
            if more:
                r_rows(nxt, 1)
                h_matmul(nxt, 1, 0)
                scale_plane(nxt, 1, 1, "S")
                h_copy(nxt, 1, 0, "S")
            out_relu(g - 1, 5)
            if more:
                scale_plane(nxt, 1, 0, "S")
            for block in range(3 if more else 2):
                out_add(g, block)
                if not more:
                    out_relu(g, block)
            a_quantise(g, 1)
            if more:
                out_add(g, 3)
        last = GRAPHS - 1
        for block in range(4, 8):
            out_matmul(last, block)
        out_relu(last - 1, 6)
        out_relu(last - 1, 7)
        for block in range(2, 8):
            out_add(last, block)
            out_relu(last, block)
